import numpy as np
import ml_dtypes


def mxq(x, axis, fmt="e4m3"):
    dtype, down = {"e4m3": (ml_dtypes.float8_e4m3fn, 7), "e5m2": (ml_dtypes.float8_e5m2, 14)}[fmt]
    v = np.moveaxis(np.asarray(x, np.float32).astype(ml_dtypes.bfloat16).astype(np.float64), axis, -1)
    blocks = v.reshape(v.shape[:-1] + (-1, 32))
    amax = np.abs(blocks).max(-1, keepdims=True)
    byte = np.maximum(np.where(amax > 0, np.frexp(amax)[1] - 1 + 127, 0) - down, 1)
    scale = np.exp2(byte - 127.0)
    codes = (blocks / scale).astype(np.float32).astype(dtype).astype(np.float64)
    return np.moveaxis((codes * scale).reshape(v.shape), -1, axis)


WIDE = False


def mx_kscale(k):
    if not WIDE:
        return np.ones(k)
    levels = np.array([10, -10, 5, -5, 0])
    if k % 512:
        return np.exp2(np.random.permutation(np.resize(levels, k // 32))).repeat(32)
    a = np.empty((k // 512, 16))
    for p in range(k // 512):
        a[p, :8] = np.random.permutation(np.resize(levels, 8))
        for g in range(8):
            far = levels[np.abs(levels - a[p, g]) >= 10]
            a[p, g + 8] = far[np.random.randint(len(far))]
    return np.exp2(a.ravel()).repeat(32)


BF16 = ml_dtypes.bfloat16


def bf(x):
    return np.asarray(x, np.float32).astype(BF16)


def f64(x):
    return np.asarray(x).astype(np.float64)


B, S, D, H, DH, F = 2, 128, 2048, 16, 128, 4096
E = H * DH
EPS = 1e-5
NTERMS = 120


def layernorm(x, g, b):
    mu = x.mean(-1, keepdims=True)
    var = np.square(x - mu).mean(-1, keepdims=True)
    return (x - mu) / np.sqrt(var + EPS) * g + b


def erf(v):
    a = np.minimum(np.maximum(v, -6.0), 6.0)
    term = a.copy()
    total = a.copy()
    for n in range(1, NTERMS):
        term = term * (2.0 * a * a) / (2.0 * n + 1.0)
        total = total + term
    return 2.0 / np.sqrt(np.pi) * np.exp(-a * a) * total


def gelu_erf(v):
    return 0.5 * v * (1.0 + erf(v / np.sqrt(2.0)))


def setup_inputs():
    s, t = mx_kscale(E), mx_kscale(D)
    x = np.random.standard_normal((B, S, D)) + 0.5 * np.random.standard_normal((B, S, 1))
    return {"h_attn": bf(0.2 * np.random.standard_normal((B, S, E)) * s),
            "x": bf(x),
            "w_out": bf(np.random.standard_normal((D, E)) * 2.0 / np.sqrt(E) / s),
            "w_fc1": bf(np.random.standard_normal((F, D)) / np.sqrt(D) / t),
            "g2": bf((1.0 + 0.1 * np.random.standard_normal(D)) * t),
            "b2": bf(0.1 * np.random.standard_normal(D) * t)}


def reference(h_attn, x, w_out, w_fc1, g2, b2):
    x_mid = f64(x) + (mxq(f64(h_attn), 2, "e4m3") @ mxq(f64(w_out), 1, "e4m3").T)
    h = layernorm(x_mid, f64(g2), f64(b2))
    u = mxq(h, 2, "e4m3") @ mxq(f64(w_fc1), 1, "e4m3").T
    return x_mid, gelu_erf(u)

@@ -1,0 +1,242 @@
+from contextlib import ExitStack
+
+import concourse.mybir as mybir
+from concourse.masks import make_identity
+
+F32 = mybir.dt.float32
+BF16 = mybir.dt.bfloat16
+U32 = mybir.dt.uint32
+U8 = mybir.dt.uint8
+FP8X4 = mybir.dt.float8_e4m3fn_x4
+ACT = mybir.ActivationFunctionType
+ALU = mybir.AluOpType
+
+P = 128
+PACK = 4
+K = 2048
+PASSES = K // (P * PACK)
+TOKENS = 256
+TOKEN_TILES = TOKENS // P
+D_MODEL = 2048
+D_FF = 4096
+BLOCK = 256
+GROUP = 512
+GROUPS_OUT = D_MODEL // GROUP
+GROUPS = GROUPS_OUT + D_FF // GROUP
+EPS = 1e-5
+
+RAW_BUFS = 10
+FIRST_SHARED_GROUP = 7
+
+FLOPS = 2 * TOKENS * K * (D_MODEL + D_FF)
+
+
+def tile_minitransformerlayer_pb_kernel(tc, h_attn, x, w_out, w_fc1, g2, b2, out_0, out_1):
+    nc = tc.nc
+    x_rows = x.flatten_outer_dims()
+    x_mid_rows = out_0.flatten_outer_dims()
+    act_rows = out_1.flatten_outer_dims()
+
+    blocks = [h_attn.flatten_outer_dims()]
+    blocks.extend([w_out[r : r + BLOCK, :] for r in range(0, D_MODEL, BLOCK)])
+    blocks.extend([w_fc1[r : r + BLOCK, :] for r in range(0, D_FF, BLOCK)])
+
+    with ExitStack() as ctx:
+        ctx.enter_context(tc.manual_schedule())
+        const = ctx.enter_context(tc.tile_pool(name="const", bufs=1))
+        raw_pool = ctx.enter_context(tc.tile_pool(name="raw", bufs=RAW_BUFS))
+        grouped_pool = ctx.enter_context(tc.tile_pool(name="grouped", bufs=10))
+        weight_pool = ctx.enter_context(tc.tile_pool(name="weights", bufs=4))
+        result_pool = ctx.enter_context(tc.tile_pool(name="result", bufs=8))
+        bank_pool = ctx.enter_context(tc.psum_pool(name="banks", bufs=6))
+        acc_pool = ctx.enter_context(tc.psum_pool(name="acc", bufs=2))
+
+        zero = const.tile([P, 1], F32)
+        nc.vector.memset(zero[:], 0.0)
+        table_warmer = const.tile([P, 1], F32)
+        nc.scalar.activation(out=table_warmer[:], in_=zero[:], func=ACT.Gelu)
+
+        ident = const.tile([P, P], F32)
+        make_identity(nc, ident[:])
+        minus_half = const.tile([P, TOKEN_TILES], F32)
+        nc.gpsimd.memset(minus_half[:], -0.5)
+
+        loaded = []
+
+        def load_next_block():
+            if len(loaded) < len(blocks):
+                raw = raw_pool.tile([P, 2, K], BF16)
+                rows = blocks[len(loaded)]
+                nc.sync.dma_start(out=raw[:], in_=rows.rearrange("(p c) k -> p c k", c=2))
+                loaded.append(raw)
+
+        gain_rows = const.tile([P, PACK * P], BF16)
+        nc.vector.memset(gain_rows[:], 0.0)
+        nc.scalar.dma_start(out=gain_rows[0:4, :], in_=g2.rearrange("(r c) -> r c", c=PACK * P))
+        nc.scalar.dma_start(out=gain_rows[4:8, :], in_=b2.rearrange("(r c) -> r c", c=PACK * P))
+
+        x_sb = const.tile([P, TOKEN_TILES, D_MODEL], BF16)
+        for b in range(RAW_BUFS):
+            load_next_block()
+            if b == 4:
+                nc.sync.dma_start(out=x_sb[:], in_=x_rows.rearrange("(t p) d -> p t d", p=P))
+
+        def quantise(grouped, codes, scales):
+            nc.vector.quantize_mx(
+                out=codes.bitcast(FP8X4),
+                scales=scales,
+                in_=grouped[:].rearrange("p n t -> p (n t)"),
+            )
+
+        def pack_block(b, codes, scales, vector_every, postponed=None):
+            words = loaded[b][:].bitcast(F32)
+            waiting = None
+            for g in range(PASSES):
+                bank = bank_pool.tile([P, 2, 2, P], F32)
+                for u in range(2):
+                    first = 2 * g * P + u
+                    for c in range(2):
+                        nc.tensor.transpose(bank[:, u, c, :], words[:, c, first : 2 * (g + 1) * P : 2], ident[:])
+                grouped = grouped_pool.tile([P, BLOCK, PACK], BF16, align_bytes=64)
+                to_words = grouped[:].bitcast(F32).rearrange("p (j c) u -> p j c u", c=2)
+                from_bank = bank[:].rearrange("p u c j -> p j c u")
+                bank_number = b * PASSES + g
+                if vector_every and bank_number % vector_every == vector_every - 1:
+                    nc.vector.tensor_copy(out=to_words, in_=from_bank)
+                else:
+                    nc.scalar.copy(out=to_words, in_=from_bank)
+                if postponed is not None:
+                    postponed.append((grouped, codes[:, g, :], scales[:, g, :]))
+                    continue
+                if waiting is not None:
+                    quantise(*waiting)
+                waiting = (grouped, codes[:, g, :], scales[:, g, :])
+            if waiting is not None:
+                quantise(*waiting)
+            load_next_block()
+
+        def prepare_group(i, postponed=None):
+            codes = weight_pool.tile([P, PASSES, GROUP], U32, align_bytes=64)
+            scales = weight_pool.tile([P, PASSES, GROUP], U8, align_bytes=64)
+            for half in range(2):
+                cols = slice(half * BLOCK, (half + 1) * BLOCK)
+                pack_block(
+                    1 + 2 * i + half,
+                    codes[:, :, cols],
+                    scales[:, :, cols],
+                    3 if i >= FIRST_SHARED_GROUP else 0,
+                    postponed,
+                )
+            return codes, scales
+
+        def mx_product(tokens, weights, tt):
+            token_codes, token_scales = tokens
+            weight_codes, weight_scales = weights
+            rows = slice(tt * P, (tt + 1) * P)
+            acc = acc_pool.tile([P, GROUP], F32)
+            for g in range(PASSES):
+                nc.tensor.matmul_mx(
+                    out=acc[:],
+                    lhsT=token_codes[:, g, rows].bitcast(FP8X4),
+                    lhsT_scale=token_scales[:, g, rows],
+                    rhs=weight_codes[:, g, :].bitcast(FP8X4),
+                    rhs_scale=weight_scales[:, g, :],
+                    start=(g == 0),
+                    stop=(g == PASSES - 1),
+                )
+            return acc
+
+        attn_codes = const.tile([P, PASSES, TOKENS], U32, align_bytes=64)
+        attn_scales = const.tile([P, PASSES, TOKENS], U8, align_bytes=64)
+        x_mid = const.tile([P, TOKEN_TILES, D_MODEL], F32)
+        stats = const.tile([P, TOKEN_TILES, GROUPS_OUT, 6], F32)
+
+        def project_group(i, weights):
+            cols = slice(i * GROUP, (i + 1) * GROUP)
+            for tt in range(TOKEN_TILES):
+                acc = mx_product((attn_codes, attn_scales), weights, tt)
+                nc.vector.tensor_tensor(out=x_mid[:, tt, cols], in0=acc[:], in1=x_sb[:, tt, cols], op=ALU.add)
+                nc.vector.bn_stats(out=stats[:, tt, i, :], in_=x_mid[:, tt, cols])
+
+        pack_block(0, attn_codes[:], attn_scales[:], 2)
+
+        bank = bank_pool.tile([P, 2, 2, P], F32)
+        for u in range(2):
+            nc.tensor.transpose(bank[:, u, 0, :], gain_rows[:].bitcast(F32)[:, u : 2 * P : 2], ident[:])
+        gain_words = const.tile([P, 2, 8], F32)
+        nc.vector.tensor_copy(out=gain_words[:], in_=bank[:, :, 0, 0:8])
+        gain_bias = const.tile([P, 2, 8, 2], F32)
+        nc.vector.tensor_copy(
+            out=gain_bias[:].rearrange("p u r e -> p (u r e)"),
+            in_=gain_words[:].rearrange("p u r -> p (u r)").bitcast(BF16),
+        )
+        gain = gain_bias[:, :, 0:4, :]
+        bias = gain_bias[:, :, 4:8, :]
+
+        prepared = {0: prepare_group(0)}
+        for i in range(1, GROUPS_OUT):
+            prepared[i] = prepare_group(i)
+            project_group(i - 1, prepared[i - 1])
+        project_group(GROUPS_OUT - 1, prepared[GROUPS_OUT - 1])
+        for tt in range(TOKEN_TILES):
+            nc.sync.dma_start(out=x_mid_rows[tt * P : (tt + 1) * P, :], in_=x_mid[:, tt, :])
+
+        mean_var = const.tile([P, TOKEN_TILES, 2], F32)
+        for tt in range(TOKEN_TILES):
+            nc.vector.bn_aggr(out=mean_var[:, tt, :], in_=stats[:, tt, :, :].rearrange("p i s -> p (i s)"))
+        var_eps = const.tile([P, TOKEN_TILES], F32)
+        nc.vector.tensor_scalar_add(out=var_eps[:], in0=mean_var[:, :, 1], scalar1=EPS)
+        rstd = const.tile([P, TOKEN_TILES], F32)
+        nc.gpsimd.tensor_tensor(out=rstd[:], in0=var_eps[:], in1=minus_half[:], op=ALU.pow)
+        z = const.tile([P, TOKEN_TILES, D_MODEL], F32)
+        for g in range(PASSES):
+            cols = slice(g * P * PACK, (g + 1) * P * PACK)
+            for tt in range(TOKEN_TILES):
+                nc.vector.tensor_scalar(
+                    out=z[:, tt, cols],
+                    in0=x_mid[:, tt, cols],
+                    scalar1=mean_var[:, tt, 0:1],
+                    scalar2=rstd[:, tt : tt + 1],
+                    op0=ALU.subtract,
+                    op1=ALU.mult,
+                )
+
+        postponed = []
+        prepared[4] = prepare_group(4, postponed)
+
+        h_codes = const.tile([P, PASSES, TOKENS], U32, align_bytes=64)
+        h_scales = const.tile([P, PASSES, TOKENS], U8, align_bytes=64)
+        h_planes = const.tile([P, PASSES, PACK, TOKENS], BF16)
+        z_by_value = z[:].rearrange("p t (q v) -> p t v q", v=PACK)
+        for g in range(PASSES):
+            for u in range(2):
+                bank = bank_pool.tile([P, 2, 2, P], F32)
+                first = g * P
+                for e in range(2):
+                    for tt in range(TOKEN_TILES):
+                        nc.tensor.transpose(bank[:, e, tt, :], z_by_value[:, tt, 2 * u + e, first : first + P], ident[:])
+                for e in range(2):
+                    plane = h_planes[:, g, 2 * u + e, :]
+                    z_t = bank[:, e, :, :].rearrange("p t j -> p (t j)")
+                    scale_ap = gain[:, u, g, e : e + 1]
+                    bias_ap = bias[:, u, g, e : e + 1]
+                    nc.scalar.activation(out=plane, in_=z_t, func=ACT.Identity, bias=bias_ap, scale=scale_ap)
+            share = len(postponed) // PASSES
+            for arguments in postponed[g * share : (g + 1) * share]:
+                quantise(*arguments)
+            grouped = grouped_pool.tile([P, BLOCK, PACK], BF16, align_bytes=64)
+            nc.vector.tensor_copy(out=grouped[:], in_=h_planes[:, g, :, :].rearrange("p t n -> p n t"))
+            quantise(grouped, h_codes[:, g, :], h_scales[:, g, :])
+
+        def mlp_group(i, weights):
+            cols = slice((i - GROUPS_OUT) * GROUP, (i - GROUPS_OUT + 1) * GROUP)
+            for tt in range(TOKEN_TILES):
+                acc = mx_product((h_codes, h_scales), weights, tt)
+                result = result_pool.tile([P, GROUP], F32)
+                nc.scalar.activation(out=result[:], in_=acc[:], func=ACT.Gelu)
+                nc.sync.dma_start(out=act_rows[tt * P : (tt + 1) * P, cols], in_=result[:])
+
+        for i in range(GROUPS_OUT + 1, GROUPS):
+            prepared[i] = prepare_group(i)
+            mlp_group(i - 1, prepared[i - 1])
+        mlp_group(GROUPS - 1, prepared[GROUPS - 1])

@@ -14,6 +14,7 @@ ALU = mybir.AluOpType
 P = 128
 PACK = 4
 K = 2048
+WORDS = K // 2
 PASSES = K // (P * PACK)
 TOKENS = 256
 TOKEN_TILES = TOKENS // P
@@ -23,10 +24,14 @@ BLOCK = 256
 GROUP = 512
 GROUPS_OUT = D_MODEL // GROUP
 GROUPS = GROUPS_OUT + D_FF // GROUP
+LAST_BLOCK = 2 * GROUPS
 EPS = 1e-5
 
-RAW_BUFS = 10
-FIRST_SHARED_GROUP = 7
+RAW_BUFS = 8
+
+ORDER_ATTN = (None, None)
+ORDER_OUT = (("V", None), ("V", "S"))
+ORDER_FC1 = (("V", "V"), ("V", "V"))
 
 FLOPS = 2 * TOKENS * K * (D_MODEL + D_FF)
 
@@ -45,9 +50,10 @@ def tile_minitransformerlayer_pb_kernel(tc, h_attn, x, w_out, w_fc1, g2, b2, out
         ctx.enter_context(tc.manual_schedule())
         const = ctx.enter_context(tc.tile_pool(name="const", bufs=1))
         raw_pool = ctx.enter_context(tc.tile_pool(name="raw", bufs=RAW_BUFS))
-        grouped_pool = ctx.enter_context(tc.tile_pool(name="grouped", bufs=10))
-        weight_pool = ctx.enter_context(tc.tile_pool(name="weights", bufs=4))
-        result_pool = ctx.enter_context(tc.tile_pool(name="result", bufs=8))
+        ordered_pool = ctx.enter_context(tc.tile_pool(name="ordered", bufs=6))
+        grouped_pool = ctx.enter_context(tc.tile_pool(name="grouped", bufs=12))
+        weight_pool = ctx.enter_context(tc.tile_pool(name="weights", bufs=5))
+        result_pool = ctx.enter_context(tc.tile_pool(name="result", bufs=6))
         bank_pool = ctx.enter_context(tc.psum_pool(name="banks", bufs=6))
         acc_pool = ctx.enter_context(tc.psum_pool(name="acc", bufs=2))
 
@@ -60,26 +66,88 @@ def tile_minitransformerlayer_pb_kernel(tc, h_attn, x, w_out, w_fc1, g2, b2, out
         make_identity(nc, ident[:])
         minus_half = const.tile([P, TOKEN_TILES], F32)
         nc.gpsimd.memset(minus_half[:], -0.5)
-
-        loaded = []
-
-        def load_next_block():
-            if len(loaded) < len(blocks):
-                raw = raw_pool.tile([P, 2, K], BF16)
-                rows = blocks[len(loaded)]
-                nc.sync.dma_start(out=raw[:], in_=rows.rearrange("(p c) k -> p c k", c=2))
-                loaded.append(raw)
-
         gain_rows = const.tile([P, PACK * P], BF16)
         nc.vector.memset(gain_rows[:], 0.0)
-        nc.scalar.dma_start(out=gain_rows[0:4, :], in_=g2.rearrange("(r c) -> r c", c=PACK * P))
-        nc.scalar.dma_start(out=gain_rows[4:8, :], in_=b2.rearrange("(r c) -> r c", c=PACK * P))
+
+        raws = {}
+
+        def load_block(b):
+            if b <= LAST_BLOCK:
+                raw = raw_pool.tile([P, 2, K], BF16)
+                nc.sync.dma_start(out=raw[:], in_=blocks[b].rearrange("(p c) k -> p c k", c=2))
+                raws[b] = raw
 
         x_sb = const.tile([P, TOKEN_TILES, D_MODEL], BF16)
         for b in range(RAW_BUFS):
-            load_next_block()
-            if b == 4:
+            load_block(b)
+            if b == 3:
                 nc.sync.dma_start(out=x_sb[:], in_=x_rows.rearrange("(t p) d -> p t d", p=P))
+        nc.sync.dma_start(out=gain_rows[0:4, :], in_=g2.rearrange("(r c) -> r c", c=PACK * P))
+        nc.sync.dma_start(out=gain_rows[4:8, :], in_=b2.rearrange("(r c) -> r c", c=PACK * P))
+
+        attn_codes = const.tile([P, PASSES, TOKENS], U32, align_bytes=64)
+        attn_scales = const.tile([P, PASSES, TOKENS], U8, align_bytes=64)
+        h_codes = const.tile([P, PASSES, TOKENS], U32, align_bytes=64)
+        h_scales = const.tile([P, PASSES, TOKENS], U8, align_bytes=64)
+        weights = {}
+
+        def destination(b):
+            if b == 0:
+                return attn_codes[:], attn_scales[:]
+            i, half = divmod(b - 1, 2)
+            if i not in weights:
+                codes = weight_pool.tile([P, PASSES, GROUP], U32, align_bytes=64)
+                scales = weight_pool.tile([P, PASSES, GROUP], U8, align_bytes=64)
+                weights[i] = (codes, scales)
+            codes, scales = weights[i]
+            cols = slice(half * BLOCK, (half + 1) * BLOCK)
+            return codes[:, :, cols], scales[:, :, cols]
+
+        sources = {}
+
+        def order_block(b):
+            if b > LAST_BLOCK:
+                return
+            if b == 0:
+                who = ORDER_ATTN
+            else:
+                who = (ORDER_OUT if b <= 2 * GROUPS_OUT else ORDER_FC1)[(b - 1) % 2]
+            words = raws[b][:].bitcast(F32)
+            views = []
+            for c in range(2):
+                by_word = words[:, c, :].rearrange("p (g w u) -> p g u w", g=PASSES, u=2)
+                if who[c] is None:
+                    views.append(by_word)
+                    continue
+                ordered = ordered_pool.tile([P, PASSES, 2, P], F32)
+                if who[c] == "V":
+                    nc.vector.tensor_copy(out=ordered[:], in_=by_word)
+                else:
+                    nc.scalar.copy(out=ordered[:], in_=by_word)
+                views.append(ordered[:])
+            sources[b] = views
+
+        waiting = {}
+
+        def transpose_block(b, vector_banks=()):
+            if b > LAST_BLOCK:
+                return
+            views = sources[b]
+            waiting[b] = []
+            for g in range(PASSES):
+                bank = bank_pool.tile([P, 2, 2, P], F32)
+                for c in range(2):
+                    for u in range(2):
+                        nc.tensor.transpose(bank[:, u, c, :], views[c][:, g, u, :], ident[:])
+                grouped = grouped_pool.tile([P, BLOCK, PACK], BF16, align_bytes=64)
+                to_words = grouped[:].bitcast(F32).rearrange("p (j c) u -> p j c u", c=2)
+                from_bank = bank[:].rearrange("p u c j -> p j c u")
+                if g in vector_banks:
+                    nc.vector.tensor_copy(out=to_words, in_=from_bank)
+                else:
+                    nc.scalar.copy(out=to_words, in_=from_bank)
+                waiting[b].append(grouped)
+            load_block(b + RAW_BUFS)
 
         def quantise(grouped, codes, scales):
             nc.vector.quantize_mx(
@@ -88,98 +156,75 @@ def tile_minitransformerlayer_pb_kernel(tc, h_attn, x, w_out, w_fc1, g2, b2, out
                 in_=grouped[:].rearrange("p n t -> p (n t)"),
             )
 
-        def pack_block(b, codes, scales, vector_every, postponed=None):
-            words = loaded[b][:].bitcast(F32)
-            waiting = None
-            for g in range(PASSES):
-                bank = bank_pool.tile([P, 2, 2, P], F32)
-                for u in range(2):
-                    first = 2 * g * P + u
-                    for c in range(2):
-                        nc.tensor.transpose(bank[:, u, c, :], words[:, c, first : 2 * (g + 1) * P : 2], ident[:])
-                grouped = grouped_pool.tile([P, BLOCK, PACK], BF16, align_bytes=64)
-                to_words = grouped[:].bitcast(F32).rearrange("p (j c) u -> p j c u", c=2)
-                from_bank = bank[:].rearrange("p u c j -> p j c u")
-                bank_number = b * PASSES + g
-                if vector_every and bank_number % vector_every == vector_every - 1:
-                    nc.vector.tensor_copy(out=to_words, in_=from_bank)
-                else:
-                    nc.scalar.copy(out=to_words, in_=from_bank)
-                if postponed is not None:
-                    postponed.append((grouped, codes[:, g, :], scales[:, g, :]))
-                    continue
-                if waiting is not None:
-                    quantise(*waiting)
-                waiting = (grouped, codes[:, g, :], scales[:, g, :])
-            if waiting is not None:
-                quantise(*waiting)
-            load_next_block()
+        def quantise_block(b, passes=range(PASSES)):
+            codes, scales = destination(b)
+            for g in passes:
+                quantise(waiting[b][g], codes[:, g, :], scales[:, g, :])
 
-        def prepare_group(i, postponed=None):
-            codes = weight_pool.tile([P, PASSES, GROUP], U32, align_bytes=64)
-            scales = weight_pool.tile([P, PASSES, GROUP], U8, align_bytes=64)
-            for half in range(2):
-                cols = slice(half * BLOCK, (half + 1) * BLOCK)
-                pack_block(
-                    1 + 2 * i + half,
-                    codes[:, :, cols],
-                    scales[:, :, cols],
-                    3 if i >= FIRST_SHARED_GROUP else 0,
-                    postponed,
-                )
-            return codes, scales
-
-        def mx_product(tokens, weights, tt):
+        def mx_product(tokens, i):
             token_codes, token_scales = tokens
-            weight_codes, weight_scales = weights
-            rows = slice(tt * P, (tt + 1) * P)
-            acc = acc_pool.tile([P, GROUP], F32)
-            for g in range(PASSES):
-                nc.tensor.matmul_mx(
-                    out=acc[:],
-                    lhsT=token_codes[:, g, rows].bitcast(FP8X4),
-                    lhsT_scale=token_scales[:, g, rows],
-                    rhs=weight_codes[:, g, :].bitcast(FP8X4),
-                    rhs_scale=weight_scales[:, g, :],
-                    start=(g == 0),
-                    stop=(g == PASSES - 1),
-                )
-            return acc
+            weight_codes, weight_scales = weights[i]
+            accs = []
+            for tt in range(TOKEN_TILES):
+                rows = slice(tt * P, (tt + 1) * P)
+                acc = acc_pool.tile([P, GROUP], F32)
+                for g in range(PASSES):
+                    nc.tensor.matmul_mx(
+                        out=acc[:],
+                        lhsT=token_codes[:, g, rows].bitcast(FP8X4),
+                        lhsT_scale=token_scales[:, g, rows],
+                        rhs=weight_codes[:, g, :].bitcast(FP8X4),
+                        rhs_scale=weight_scales[:, g, :],
+                        start=(g == 0),
+                        stop=(g == PASSES - 1),
+                    )
+                accs.append(acc)
+            return accs
 
-        attn_codes = const.tile([P, PASSES, TOKENS], U32, align_bytes=64)
-        attn_scales = const.tile([P, PASSES, TOKENS], U8, align_bytes=64)
         x_mid = const.tile([P, TOKEN_TILES, D_MODEL], F32)
         stats = const.tile([P, TOKEN_TILES, GROUPS_OUT, 6], F32)
 
-        def project_group(i, weights):
+        def project_group(i):
             cols = slice(i * GROUP, (i + 1) * GROUP)
+            accs = mx_product((attn_codes, attn_scales), i)
             for tt in range(TOKEN_TILES):
-                acc = mx_product((attn_codes, attn_scales), weights, tt)
-                nc.vector.tensor_tensor(out=x_mid[:, tt, cols], in0=acc[:], in1=x_sb[:, tt, cols], op=ALU.add)
+                nc.vector.tensor_tensor(out=x_mid[:, tt, cols], in0=accs[tt][:], in1=x_sb[:, tt, cols], op=ALU.add)
+            for tt in range(TOKEN_TILES):
                 nc.vector.bn_stats(out=stats[:, tt, i, :], in_=x_mid[:, tt, cols])
 
-        pack_block(0, attn_codes[:], attn_scales[:], 2)
+        def mlp_group(i):
+            cols = slice((i - GROUPS_OUT) * GROUP, (i - GROUPS_OUT + 1) * GROUP)
+            accs = mx_product((h_codes, h_scales), i)
+            for tt in range(TOKEN_TILES):
+                result = result_pool.tile([P, GROUP], F32)
+                nc.scalar.activation(out=result[:], in_=accs[tt][:], func=ACT.Gelu)
+                nc.sync.dma_start(out=act_rows[tt * P : (tt + 1) * P, cols], in_=result[:])
+
+        order_block(0)
+        order_block(1)
+        transpose_block(0)
+        order_block(2)
+        transpose_block(1)
+        quantise_block(0)
+        last_out = 2 * GROUPS_OUT
+        for b in range(1, last_out + 1):
+            order_block(b + 2)
+            transpose_block(b + 1)
+            quantise_block(b)
+            if b % 2 == 1 and b >= 3:
+                project_group((b - 3) // 2)
 
         bank = bank_pool.tile([P, 2, 2, P], F32)
         for u in range(2):
             nc.tensor.transpose(bank[:, u, 0, :], gain_rows[:].bitcast(F32)[:, u : 2 * P : 2], ident[:])
         gain_words = const.tile([P, 2, 8], F32)
-        nc.vector.tensor_copy(out=gain_words[:], in_=bank[:, :, 0, 0:8])
-        gain_bias = const.tile([P, 2, 8, 2], F32)
-        nc.vector.tensor_copy(
-            out=gain_bias[:].rearrange("p u r e -> p (u r e)"),
-            in_=gain_words[:].rearrange("p u r -> p (u r)").bitcast(BF16),
-        )
-        gain = gain_bias[:, :, 0:4, :]
-        bias = gain_bias[:, :, 4:8, :]
+        nc.scalar.copy(out=gain_words[:], in_=bank[:, :, 0, 0:8])
 
-        prepared = {0: prepare_group(0)}
-        for i in range(1, GROUPS_OUT):
-            prepared[i] = prepare_group(i)
-            project_group(i - 1, prepared[i - 1])
-        project_group(GROUPS_OUT - 1, prepared[GROUPS_OUT - 1])
+        project_group(GROUPS_OUT - 1)
         for tt in range(TOKEN_TILES):
             nc.sync.dma_start(out=x_mid_rows[tt * P : (tt + 1) * P, :], in_=x_mid[:, tt, :])
+
+        transpose_block(last_out + 2)
 
         mean_var = const.tile([P, TOKEN_TILES, 2], F32)
         for tt in range(TOKEN_TILES):
@@ -188,55 +233,59 @@ def tile_minitransformerlayer_pb_kernel(tc, h_attn, x, w_out, w_fc1, g2, b2, out
         nc.vector.tensor_scalar_add(out=var_eps[:], in0=mean_var[:, :, 1], scalar1=EPS)
         rstd = const.tile([P, TOKEN_TILES], F32)
         nc.gpsimd.tensor_tensor(out=rstd[:], in0=var_eps[:], in1=minus_half[:], op=ALU.pow)
-        z = const.tile([P, TOKEN_TILES, D_MODEL], F32)
+        gain_bias = const.tile([P, 2, 8, 2], F32)
+        nc.vector.tensor_copy(
+            out=gain_bias[:].rearrange("p u r e -> p (u r e)"),
+            in_=gain_words[:].rearrange("p u r -> p (u r)").bitcast(BF16),
+        )
+        gain = gain_bias[:, :, 0:4, :]
+        bias = gain_bias[:, :, 4:8, :]
+        quantise_block(last_out + 1)
+        z = const.tile([P, TOKEN_TILES, PASSES, PACK, P], F32)
         for g in range(PASSES):
             cols = slice(g * P * PACK, (g + 1) * P * PACK)
             for tt in range(TOKEN_TILES):
                 nc.vector.tensor_scalar(
-                    out=z[:, tt, cols],
-                    in0=x_mid[:, tt, cols],
+                    out=z[:, tt, g, :, :],
+                    in0=x_mid[:, tt, cols].rearrange("p (q t) -> p t q", t=PACK),
                     scalar1=mean_var[:, tt, 0:1],
                     scalar2=rstd[:, tt : tt + 1],
                     op0=ALU.subtract,
                     op1=ALU.mult,
                 )
+        order_block(last_out + 3)
 
-        postponed = []
-        prepared[4] = prepare_group(4, postponed)
-
-        h_codes = const.tile([P, PASSES, TOKENS], U32, align_bytes=64)
-        h_scales = const.tile([P, PASSES, TOKENS], U8, align_bytes=64)
         h_planes = const.tile([P, PASSES, PACK, TOKENS], BF16)
-        z_by_value = z[:].rearrange("p t (q v) -> p t v q", v=PACK)
         for g in range(PASSES):
             for u in range(2):
                 bank = bank_pool.tile([P, 2, 2, P], F32)
-                first = g * P
                 for e in range(2):
                     for tt in range(TOKEN_TILES):
-                        nc.tensor.transpose(bank[:, e, tt, :], z_by_value[:, tt, 2 * u + e, first : first + P], ident[:])
+                        nc.tensor.transpose(bank[:, e, tt, :], z[:, tt, g, 2 * u + e, :], ident[:])
                 for e in range(2):
-                    plane = h_planes[:, g, 2 * u + e, :]
-                    z_t = bank[:, e, :, :].rearrange("p t j -> p (t j)")
-                    scale_ap = gain[:, u, g, e : e + 1]
-                    bias_ap = bias[:, u, g, e : e + 1]
-                    nc.scalar.activation(out=plane, in_=z_t, func=ACT.Identity, bias=bias_ap, scale=scale_ap)
-            share = len(postponed) // PASSES
-            for arguments in postponed[g * share : (g + 1) * share]:
-                quantise(*arguments)
+                    nc.scalar.activation(
+                        out=h_planes[:, g, 2 * u + e, :],
+                        in_=bank[:, e, :, :].rearrange("p t j -> p (t j)"),
+                        func=ACT.Identity,
+                        bias=bias[:, u, g, e : e + 1],
+                        scale=gain[:, u, g, e : e + 1],
+                    )
+        transpose_block(last_out + 3)
+        h_grouped = []
+        for g in range(PASSES):
+            quantise_block(last_out + 2, [g])
             grouped = grouped_pool.tile([P, BLOCK, PACK], BF16, align_bytes=64)
             nc.vector.tensor_copy(out=grouped[:], in_=h_planes[:, g, :, :].rearrange("p t n -> p n t"))
-            quantise(grouped, h_codes[:, g, :], h_scales[:, g, :])
+            h_grouped.append(grouped)
+            if g > 0:
+                quantise(h_grouped[g - 1], h_codes[:, g - 1, :], h_scales[:, g - 1, :])
+        order_block(last_out + 4)
+        quantise(h_grouped[PASSES - 1], h_codes[:, PASSES - 1, :], h_scales[:, PASSES - 1, :])
 
-        def mlp_group(i, weights):
-            cols = slice((i - GROUPS_OUT) * GROUP, (i - GROUPS_OUT + 1) * GROUP)
-            for tt in range(TOKEN_TILES):
-                acc = mx_product((h_codes, h_scales), weights, tt)
-                result = result_pool.tile([P, GROUP], F32)
-                nc.scalar.activation(out=result[:], in_=acc[:], func=ACT.Gelu)
-                nc.sync.dma_start(out=act_rows[tt * P : (tt + 1) * P, cols], in_=result[:])
-
-        for i in range(GROUPS_OUT + 1, GROUPS):
-            prepared[i] = prepare_group(i)
-            mlp_group(i - 1, prepared[i - 1])
-        mlp_group(GROUPS - 1, prepared[GROUPS - 1])
+        for b in range(last_out + 3, LAST_BLOCK + 1):
+            order_block(b + 2)
+            transpose_block(b + 1, (1,) if b % 2 == 1 else ())
+            quantise_block(b)
+            if b % 2 == 1:
+                mlp_group((b - 3) // 2)
+        mlp_group(GROUPS - 1)

@@ -29,10 +29,6 @@ EPS = 1e-5
 
 RAW_BUFS = 8
 
-ORDER_ATTN = (None, None)
-ORDER_OUT = (("V", None), ("V", "S"))
-ORDER_FC1 = (("V", "V"), ("V", "V"))
-
 FLOPS = 2 * TOKENS * K * (D_MODEL + D_FF)
 
 
@@ -108,22 +104,17 @@ def tile_minitransformerlayer_pb_kernel(tc, h_attn, x, w_out, w_fc1, g2, b2, out
         def order_block(b):
             if b > LAST_BLOCK:
                 return
-            if b == 0:
-                who = ORDER_ATTN
-            else:
-                who = (ORDER_OUT if b <= 2 * GROUPS_OUT else ORDER_FC1)[(b - 1) % 2]
             words = raws[b][:].bitcast(F32)
             views = []
             for c in range(2):
-                by_word = words[:, c, :].rearrange("p (g w u) -> p g u w", g=PASSES, u=2)
-                if who[c] is None:
-                    views.append(by_word)
+                if b <= 2 * GROUPS_OUT:
+                    views.append(words[:, c, :].rearrange("p (g w u) -> p g u w", g=PASSES, u=2))
                     continue
                 ordered = ordered_pool.tile([P, PASSES, 2, P], F32)
-                if who[c] == "V":
-                    nc.vector.tensor_copy(out=ordered[:], in_=by_word)
-                else:
-                    nc.scalar.copy(out=ordered[:], in_=by_word)
+                nc.vector.tensor_copy(
+                    out=ordered[:].rearrange("p g u (q i) -> p g u q i", i=8),
+                    in_=words[:, c, :].rearrange("p (g q u i) -> p g u q i", g=PASSES, u=2, i=8),
+                )
                 views.append(ordered[:])
             sources[b] = views
 
@@ -161,44 +152,38 @@ def tile_minitransformerlayer_pb_kernel(tc, h_attn, x, w_out, w_fc1, g2, b2, out
             for g in passes:
                 quantise(waiting[b][g], codes[:, g, :], scales[:, g, :])
 
-        def mx_product(tokens, i):
+        def mx_product(tokens, i, tt):
             token_codes, token_scales = tokens
             weight_codes, weight_scales = weights[i]
-            accs = []
-            for tt in range(TOKEN_TILES):
-                rows = slice(tt * P, (tt + 1) * P)
-                acc = acc_pool.tile([P, GROUP], F32)
-                for g in range(PASSES):
-                    nc.tensor.matmul_mx(
-                        out=acc[:],
-                        lhsT=token_codes[:, g, rows].bitcast(FP8X4),
-                        lhsT_scale=token_scales[:, g, rows],
-                        rhs=weight_codes[:, g, :].bitcast(FP8X4),
-                        rhs_scale=weight_scales[:, g, :],
-                        start=(g == 0),
-                        stop=(g == PASSES - 1),
-                    )
-                accs.append(acc)
-            return accs
+            rows = slice(tt * P, (tt + 1) * P)
+            acc = acc_pool.tile([P, GROUP], F32)
+            for g in range(PASSES):
+                nc.tensor.matmul_mx(
+                    out=acc[:],
+                    lhsT=token_codes[:, g, rows].bitcast(FP8X4),
+                    lhsT_scale=token_scales[:, g, rows],
+                    rhs=weight_codes[:, g, :].bitcast(FP8X4),
+                    rhs_scale=weight_scales[:, g, :],
+                    start=(g == 0),
+                    stop=(g == PASSES - 1),
+                )
+            return acc
 
         x_mid = const.tile([P, TOKEN_TILES, D_MODEL], F32)
         stats = const.tile([P, TOKEN_TILES, GROUPS_OUT, 6], F32)
 
-        def project_group(i):
+        def project(i, tt):
             cols = slice(i * GROUP, (i + 1) * GROUP)
-            accs = mx_product((attn_codes, attn_scales), i)
-            for tt in range(TOKEN_TILES):
-                nc.vector.tensor_tensor(out=x_mid[:, tt, cols], in0=accs[tt][:], in1=x_sb[:, tt, cols], op=ALU.add)
-            for tt in range(TOKEN_TILES):
-                nc.vector.bn_stats(out=stats[:, tt, i, :], in_=x_mid[:, tt, cols])
+            acc = mx_product((attn_codes, attn_scales), i, tt)
+            nc.vector.tensor_tensor(out=x_mid[:, tt, cols], in0=acc[:], in1=x_sb[:, tt, cols], op=ALU.add)
+            nc.vector.bn_stats(out=stats[:, tt, i, :], in_=x_mid[:, tt, cols])
 
-        def mlp_group(i):
+        def mlp(i, tt):
             cols = slice((i - GROUPS_OUT) * GROUP, (i - GROUPS_OUT + 1) * GROUP)
-            accs = mx_product((h_codes, h_scales), i)
-            for tt in range(TOKEN_TILES):
-                result = result_pool.tile([P, GROUP], F32)
-                nc.scalar.activation(out=result[:], in_=accs[tt][:], func=ACT.Gelu)
-                nc.sync.dma_start(out=act_rows[tt * P : (tt + 1) * P, cols], in_=result[:])
+            acc = mx_product((h_codes, h_scales), i, tt)
+            result = result_pool.tile([P, GROUP], F32)
+            nc.scalar.activation(out=result[:], in_=acc[:], func=ACT.Gelu)
+            nc.sync.dma_start(out=act_rows[tt * P : (tt + 1) * P, cols], in_=result[:])
 
         order_block(0)
         order_block(1)
@@ -211,16 +196,22 @@ def tile_minitransformerlayer_pb_kernel(tc, h_attn, x, w_out, w_fc1, g2, b2, out
             order_block(b + 2)
             transpose_block(b + 1)
             quantise_block(b)
-            if b % 2 == 1 and b >= 3:
-                project_group((b - 3) // 2)
+            if b >= 3:
+                project((b - 3) // 2, (b - 3) % 2)
 
+        gain_ordered = const.tile([P, 2, P], F32)
+        nc.vector.tensor_copy(
+            out=gain_ordered[:].rearrange("p u (q i) -> p u q i", i=8),
+            in_=gain_rows[:].bitcast(F32).rearrange("p (q u i) -> p u q i", u=2, i=8),
+        )
         bank = bank_pool.tile([P, 2, 2, P], F32)
         for u in range(2):
-            nc.tensor.transpose(bank[:, u, 0, :], gain_rows[:].bitcast(F32)[:, u : 2 * P : 2], ident[:])
+            nc.tensor.transpose(bank[:, u, 0, :], gain_ordered[:, u, :], ident[:])
         gain_words = const.tile([P, 2, 8], F32)
         nc.scalar.copy(out=gain_words[:], in_=bank[:, :, 0, 0:8])
 
-        project_group(GROUPS_OUT - 1)
+        for tt in range(TOKEN_TILES):
+            project(GROUPS_OUT - 1, tt)
         for tt in range(TOKEN_TILES):
             nc.sync.dma_start(out=x_mid_rows[tt * P : (tt + 1) * P, :], in_=x_mid[:, tt, :])
 
@@ -241,13 +232,13 @@ def tile_minitransformerlayer_pb_kernel(tc, h_attn, x, w_out, w_fc1, g2, b2, out
         gain = gain_bias[:, :, 0:4, :]
         bias = gain_bias[:, :, 4:8, :]
         quantise_block(last_out + 1)
-        z = const.tile([P, TOKEN_TILES, PASSES, PACK, P], F32)
+        z = const.tile([P, TOKEN_TILES, PASSES, 2, 2 * P], F32)
         for g in range(PASSES):
             cols = slice(g * P * PACK, (g + 1) * P * PACK)
             for tt in range(TOKEN_TILES):
                 nc.vector.tensor_scalar(
-                    out=z[:, tt, g, :, :],
-                    in0=x_mid[:, tt, cols].rearrange("p (q t) -> p t q", t=PACK),
+                    out=z[:, tt, g, :, :].rearrange("p u (q r) -> p u q r", r=16),
+                    in0=x_mid[:, tt, cols].rearrange("p (q u r) -> p u q r", u=2, r=16),
                     scalar1=mean_var[:, tt, 0:1],
                     scalar2=rstd[:, tt : tt + 1],
                     op0=ALU.subtract,
@@ -261,7 +252,7 @@ def tile_minitransformerlayer_pb_kernel(tc, h_attn, x, w_out, w_fc1, g2, b2, out
                 bank = bank_pool.tile([P, 2, 2, P], F32)
                 for e in range(2):
                     for tt in range(TOKEN_TILES):
-                        nc.tensor.transpose(bank[:, e, tt, :], z[:, tt, g, 2 * u + e, :], ident[:])
+                        nc.tensor.transpose(bank[:, e, tt, :], z[:, tt, g, u, e : 2 * P : 2], ident[:])
                 for e in range(2):
                     nc.scalar.activation(
                         out=h_planes[:, g, 2 * u + e, :],
@@ -284,8 +275,10 @@ def tile_minitransformerlayer_pb_kernel(tc, h_attn, x, w_out, w_fc1, g2, b2, out
 
         for b in range(last_out + 3, LAST_BLOCK + 1):
             order_block(b + 2)
-            transpose_block(b + 1, (1,) if b % 2 == 1 else ())
+            transpose_block(b + 1, (1,) if b % 4 == 1 else ())
             quantise_block(b)
             if b % 2 == 1:
-                mlp_group((b - 3) // 2)
-        mlp_group(GROUPS - 1)
+                for tt in range(TOKEN_TILES):
+                    mlp((b - 3) // 2, tt)
+        for tt in range(TOKEN_TILES):
+            mlp(GROUPS - 1, tt)

@@ -277,8 +277,6 @@ def tile_minitransformerlayer_pb_kernel(tc, h_attn, x, w_out, w_fc1, g2, b2, out
             order_block(b + 2)
             transpose_block(b + 1, (1,) if b % 4 == 1 else ())
             quantise_block(b)
-            if b % 2 == 1:
-                for tt in range(TOKEN_TILES):
-                    mlp((b - 3) // 2, tt)
+            mlp((b - 3) // 2, (b - 3) % 2)
         for tt in range(TOKEN_TILES):
             mlp(GROUPS - 1, tt)

@@ -14,7 +14,6 @@ ALU = mybir.AluOpType
 P = 128
 PACK = 4
 K = 2048
-WORDS = K // 2
 PASSES = K // (P * PACK)
 TOKENS = 256
 TOKEN_TILES = TOKENS // P
@@ -24,10 +23,13 @@ BLOCK = 256
 GROUP = 512
 GROUPS_OUT = D_MODEL // GROUP
 GROUPS = GROUPS_OUT + D_FF // GROUP
+LAST_OUT = 2 * GROUPS_OUT
 LAST_BLOCK = 2 * GROUPS
 EPS = 1e-5
 
 RAW_BUFS = 8
+OUT_AS_IT_LIES = 4
+FC1_AS_IT_LIES = 1
 
 FLOPS = 2 * TOKENS * K * (D_MODEL + D_FF)
 
@@ -46,10 +48,10 @@ def tile_minitransformerlayer_pb_kernel(tc, h_attn, x, w_out, w_fc1, g2, b2, out
         ctx.enter_context(tc.manual_schedule())
         const = ctx.enter_context(tc.tile_pool(name="const", bufs=1))
         raw_pool = ctx.enter_context(tc.tile_pool(name="raw", bufs=RAW_BUFS))
-        ordered_pool = ctx.enter_context(tc.tile_pool(name="ordered", bufs=6))
-        grouped_pool = ctx.enter_context(tc.tile_pool(name="grouped", bufs=12))
-        weight_pool = ctx.enter_context(tc.tile_pool(name="weights", bufs=5))
-        result_pool = ctx.enter_context(tc.tile_pool(name="result", bufs=6))
+        ordered_pool = ctx.enter_context(tc.tile_pool(name="ordered", bufs=3))
+        grouped_pool = ctx.enter_context(tc.tile_pool(name="grouped", bufs=8))
+        weight_pool = ctx.enter_context(tc.tile_pool(name="weights", bufs=4))
+        result_pool = ctx.enter_context(tc.tile_pool(name="result", bufs=4))
         bank_pool = ctx.enter_context(tc.psum_pool(name="banks", bufs=6))
         acc_pool = ctx.enter_context(tc.psum_pool(name="acc", bufs=2))
 
@@ -76,146 +78,154 @@ def tile_minitransformerlayer_pb_kernel(tc, h_attn, x, w_out, w_fc1, g2, b2, out
         x_sb = const.tile([P, TOKEN_TILES, D_MODEL], BF16)
         for b in range(RAW_BUFS):
             load_block(b)
-            if b == 3:
-                nc.sync.dma_start(out=x_sb[:], in_=x_rows.rearrange("(t p) d -> p t d", p=P))
+            if b >= 3 and b - 3 < GROUPS_OUT:
+                cols = slice((b - 3) * GROUP, (b - 2) * GROUP)
+                nc.sync.dma_start(out=x_sb[:, :, cols], in_=x_rows[:, cols].rearrange("(t p) d -> p t d", p=P))
         nc.sync.dma_start(out=gain_rows[0:4, :], in_=g2.rearrange("(r c) -> r c", c=PACK * P))
         nc.sync.dma_start(out=gain_rows[4:8, :], in_=b2.rearrange("(r c) -> r c", c=PACK * P))
+
+        sources = {}
+
+        def order_block(b, engine="V"):
+            if b > LAST_BLOCK:
+                return
+            words = raws[b][:].bitcast(F32)
+            first = OUT_AS_IT_LIES if b <= LAST_OUT else FC1_AS_IT_LIES
+            as_it_lies = words.rearrange("p c (g w u) -> p u c g w", g=PASSES, u=2)
+            sources[b] = [as_it_lies[:, :, :, g, :] for g in range(first)]
+            if first == PASSES:
+                return
+            ordered = ordered_pool.tile([P, 2, 2, PASSES - first, P], F32)
+            to_runs = ordered[:].rearrange("p u c g (q i) -> p u c (g q) i", i=8)
+            from_runs = words[:, :, first * 2 * P :].rearrange("p c (a u i) -> p u c a i", u=2, i=8)
+            if engine == "V":
+                nc.vector.tensor_copy(out=to_runs, in_=from_runs)
+            else:
+                nc.scalar.copy(out=to_runs, in_=from_runs)
+            sources[b].extend([ordered[:, :, :, g, :] for g in range(PASSES - first)])
+
+        grouped_tiles = {}
+
+        def transpose_block(b, passes=range(PASSES), vector_passes=()):
+            if b > LAST_BLOCK:
+                return
+            i, half = divmod(b - 1, 2)
+            for g in passes:
+                bank = bank_pool.tile([P, 2, 2, P], F32)
+                for c in range(2):
+                    for u in range(2):
+                        nc.tensor.transpose(bank[:, u, c, :], sources[b][g][:, u, c, :], ident[:])
+                if (i, g) not in grouped_tiles:
+                    grouped = grouped_pool.tile([P, GROUP, PACK], BF16, align_bytes=64)
+                    grouped_tiles[i, g] = grouped
+                start = half * BLOCK if b > 0 else 0
+                columns = grouped_tiles[i, g][:, start : start + BLOCK, :]
+                to_words = columns.bitcast(F32).rearrange("p (j c) u -> p j c u", c=2)
+                from_bank = bank[:].rearrange("p u c j -> p j c u")
+                if g in vector_passes:
+                    nc.vector.tensor_copy(out=to_words, in_=from_bank)
+                else:
+                    nc.scalar.copy(out=to_words, in_=from_bank)
+            if PASSES - 1 in passes:
+                load_block(b + RAW_BUFS)
+
+        def quantise(grouped, codes, scales):
+            nc.vector.quantize_mx(out=codes.bitcast(FP8X4), scales=scales, in_=grouped.rearrange("p n t -> p (n t)"))
+
+        weights = {}
+
+        def quantise_group(i, passes=range(PASSES)):
+            if i not in weights:
+                weight_codes = weight_pool.tile([P, PASSES, GROUP], U32, align_bytes=64)
+                weight_scales = weight_pool.tile([P, PASSES, GROUP], U8, align_bytes=64)
+                weights[i] = (weight_codes, weight_scales)
+            codes, scales = weights[i]
+            for g in passes:
+                quantise(grouped_tiles[i, g][:], codes[:, g, :], scales[:, g, :])
 
         attn_codes = const.tile([P, PASSES, TOKENS], U32, align_bytes=64)
         attn_scales = const.tile([P, PASSES, TOKENS], U8, align_bytes=64)
         h_codes = const.tile([P, PASSES, TOKENS], U32, align_bytes=64)
         h_scales = const.tile([P, PASSES, TOKENS], U8, align_bytes=64)
-        weights = {}
 
-        def destination(b):
-            if b == 0:
-                return attn_codes[:], attn_scales[:]
-            i, half = divmod(b - 1, 2)
-            if i not in weights:
-                codes = weight_pool.tile([P, PASSES, GROUP], U32, align_bytes=64)
-                scales = weight_pool.tile([P, PASSES, GROUP], U8, align_bytes=64)
-                weights[i] = (codes, scales)
-            codes, scales = weights[i]
-            cols = slice(half * BLOCK, (half + 1) * BLOCK)
-            return codes[:, :, cols], scales[:, :, cols]
-
-        sources = {}
-
-        def order_block(b):
-            if b > LAST_BLOCK:
-                return
-            words = raws[b][:].bitcast(F32)
-            views = []
-            for c in range(2):
-                if b <= 2 * GROUPS_OUT:
-                    views.append(words[:, c, :].rearrange("p (g w u) -> p g u w", g=PASSES, u=2))
-                    continue
-                ordered = ordered_pool.tile([P, PASSES, 2, P], F32)
-                nc.vector.tensor_copy(
-                    out=ordered[:].rearrange("p g u (q i) -> p g u q i", i=8),
-                    in_=words[:, c, :].rearrange("p (g q u i) -> p g u q i", g=PASSES, u=2, i=8),
-                )
-                views.append(ordered[:])
-            sources[b] = views
-
-        waiting = {}
-
-        def transpose_block(b, vector_banks=()):
-            if b > LAST_BLOCK:
-                return
-            views = sources[b]
-            waiting[b] = []
-            for g in range(PASSES):
-                bank = bank_pool.tile([P, 2, 2, P], F32)
-                for c in range(2):
-                    for u in range(2):
-                        nc.tensor.transpose(bank[:, u, c, :], views[c][:, g, u, :], ident[:])
-                grouped = grouped_pool.tile([P, BLOCK, PACK], BF16, align_bytes=64)
-                to_words = grouped[:].bitcast(F32).rearrange("p (j c) u -> p j c u", c=2)
-                from_bank = bank[:].rearrange("p u c j -> p j c u")
-                if g in vector_banks:
-                    nc.vector.tensor_copy(out=to_words, in_=from_bank)
-                else:
-                    nc.scalar.copy(out=to_words, in_=from_bank)
-                waiting[b].append(grouped)
-            load_block(b + RAW_BUFS)
-
-        def quantise(grouped, codes, scales):
-            nc.vector.quantize_mx(
-                out=codes.bitcast(FP8X4),
-                scales=scales,
-                in_=grouped[:].rearrange("p n t -> p (n t)"),
-            )
-
-        def quantise_block(b, passes=range(PASSES)):
-            codes, scales = destination(b)
-            for g in passes:
-                quantise(waiting[b][g], codes[:, g, :], scales[:, g, :])
-
-        def mx_product(tokens, i, tt):
+        def mx_pass(acc, tokens, i, tt, g):
             token_codes, token_scales = tokens
             weight_codes, weight_scales = weights[i]
             rows = slice(tt * P, (tt + 1) * P)
-            acc = acc_pool.tile([P, GROUP], F32)
-            for g in range(PASSES):
-                nc.tensor.matmul_mx(
-                    out=acc[:],
-                    lhsT=token_codes[:, g, rows].bitcast(FP8X4),
-                    lhsT_scale=token_scales[:, g, rows],
-                    rhs=weight_codes[:, g, :].bitcast(FP8X4),
-                    rhs_scale=weight_scales[:, g, :],
-                    start=(g == 0),
-                    stop=(g == PASSES - 1),
-                )
-            return acc
+            nc.tensor.matmul_mx(
+                out=acc[:],
+                lhsT=token_codes[:, g, rows].bitcast(FP8X4),
+                lhsT_scale=token_scales[:, g, rows],
+                rhs=weight_codes[:, g, :].bitcast(FP8X4),
+                rhs_scale=weight_scales[:, g, :],
+                start=(g == 0),
+                stop=(g == PASSES - 1),
+            )
 
         x_mid = const.tile([P, TOKEN_TILES, D_MODEL], F32)
         stats = const.tile([P, TOKEN_TILES, GROUPS_OUT, 6], F32)
 
         def project(i, tt):
             cols = slice(i * GROUP, (i + 1) * GROUP)
-            acc = mx_product((attn_codes, attn_scales), i, tt)
+            acc = acc_pool.tile([P, GROUP], F32)
+            for g in range(PASSES):
+                mx_pass(acc, (attn_codes, attn_scales), i, tt, g)
             nc.vector.tensor_tensor(out=x_mid[:, tt, cols], in0=acc[:], in1=x_sb[:, tt, cols], op=ALU.add)
-            nc.vector.bn_stats(out=stats[:, tt, i, :], in_=x_mid[:, tt, cols])
 
-        def mlp(i, tt):
+        def measure(i, tt):
+            nc.vector.bn_stats(out=stats[:, tt, i, :], in_=x_mid[:, tt, i * GROUP : (i + 1) * GROUP])
+
+        def mlp(i):
             cols = slice((i - GROUPS_OUT) * GROUP, (i - GROUPS_OUT + 1) * GROUP)
-            acc = mx_product((h_codes, h_scales), i, tt)
-            result = result_pool.tile([P, GROUP], F32)
-            nc.scalar.activation(out=result[:], in_=acc[:], func=ACT.Gelu)
-            nc.sync.dma_start(out=act_rows[tt * P : (tt + 1) * P, cols], in_=result[:])
+            for tt in range(TOKEN_TILES):
+                acc = acc_pool.tile([P, GROUP], F32)
+                for g in range(PASSES):
+                    mx_pass(acc, (h_codes, h_scales), i, tt, g)
+                result = result_pool.tile([P, GROUP], F32)
+                nc.scalar.activation(out=result[:], in_=acc[:], func=ACT.Gelu)
+                nc.sync.dma_start(out=act_rows[tt * P : (tt + 1) * P, cols], in_=result[:])
 
         order_block(0)
-        order_block(1)
         transpose_block(0)
-        order_block(2)
-        transpose_block(1)
-        quantise_block(0)
-        last_out = 2 * GROUPS_OUT
-        for b in range(1, last_out + 1):
-            order_block(b + 2)
+        order_block(1)
+        for g in range(PASSES):
+            quantise(grouped_tiles[-1, g][:, :BLOCK, :], attn_codes[:, g, :], attn_scales[:, g, :])
+        for i in range(GROUPS_OUT + 1):
+            b = 2 * i + 1
+            transpose_block(b)
+            order_block(b + 1)
+            if i > 0:
+                quantise_group(i - 1)
+            if i > 1:
+                for tt in range(TOKEN_TILES):
+                    measure(i - 2, tt)
             transpose_block(b + 1)
-            quantise_block(b)
-            if b >= 3:
-                project((b - 3) // 2, (b - 3) % 2)
-
-        gain_ordered = const.tile([P, 2, P], F32)
-        nc.vector.tensor_copy(
-            out=gain_ordered[:].rearrange("p u (q i) -> p u q i", i=8),
-            in_=gain_rows[:].bitcast(F32).rearrange("p (q u i) -> p u q i", u=2, i=8),
-        )
-        bank = bank_pool.tile([P, 2, 2, P], F32)
-        for u in range(2):
-            nc.tensor.transpose(bank[:, u, 0, :], gain_ordered[:, u, :], ident[:])
-        gain_words = const.tile([P, 2, 8], F32)
-        nc.scalar.copy(out=gain_words[:], in_=bank[:, :, 0, 0:8])
-
+            order_block(b + 2, "S")
+            if i > 0:
+                for tt in range(TOKEN_TILES):
+                    project(i - 1, tt)
+            if i == 2:
+                gain_ordered = const.tile([P, 2, P], F32)
+                nc.vector.tensor_copy(
+                    out=gain_ordered[:].rearrange("p u (q i) -> p u q i", i=8),
+                    in_=gain_rows[:].bitcast(F32).rearrange("p (q u i) -> p u q i", u=2, i=8),
+                )
+            if i == 3:
+                bank = bank_pool.tile([P, 2, 2, P], F32)
+                for u in range(2):
+                    nc.tensor.transpose(bank[:, 0, u, :], gain_rows[:].bitcast(F32)[:, u : 2 * P : 2], ident[:])
+                    nc.tensor.transpose(bank[:, 1, u, :], gain_ordered[:, u, :], ident[:])
+                gain_words = const.tile([P, 2, 2, 8], F32)
+                nc.scalar.copy(out=gain_words[:], in_=bank[:, :, :, 0:8])
+                gain_bias = const.tile([P, 2, 2, 8, 2], F32)
+                nc.vector.tensor_copy(
+                    out=gain_bias[:].rearrange("p o u r e -> p (o u r e)"),
+                    in_=gain_words[:].rearrange("p o u r -> p (o u r)").bitcast(BF16),
+                )
         for tt in range(TOKEN_TILES):
-            project(GROUPS_OUT - 1, tt)
+            measure(GROUPS_OUT - 1, tt)
         for tt in range(TOKEN_TILES):
             nc.sync.dma_start(out=x_mid_rows[tt * P : (tt + 1) * P, :], in_=x_mid[:, tt, :])
-
-        transpose_block(last_out + 2)
 
         mean_var = const.tile([P, TOKEN_TILES, 2], F32)
         for tt in range(TOKEN_TILES):
@@ -224,30 +234,26 @@ def tile_minitransformerlayer_pb_kernel(tc, h_attn, x, w_out, w_fc1, g2, b2, out
         nc.vector.tensor_scalar_add(out=var_eps[:], in0=mean_var[:, :, 1], scalar1=EPS)
         rstd = const.tile([P, TOKEN_TILES], F32)
         nc.gpsimd.tensor_tensor(out=rstd[:], in0=var_eps[:], in1=minus_half[:], op=ALU.pow)
-        gain_bias = const.tile([P, 2, 8, 2], F32)
-        nc.vector.tensor_copy(
-            out=gain_bias[:].rearrange("p u r e -> p (u r e)"),
-            in_=gain_words[:].rearrange("p u r -> p (u r)").bitcast(BF16),
-        )
-        gain = gain_bias[:, :, 0:4, :]
-        bias = gain_bias[:, :, 4:8, :]
-        quantise_block(last_out + 1)
+        order_block(LAST_OUT + 4)
+
         z = const.tile([P, TOKEN_TILES, PASSES, 2, 2 * P], F32)
         for g in range(PASSES):
+            run = 2 if g < FC1_AS_IT_LIES else 16
             cols = slice(g * P * PACK, (g + 1) * P * PACK)
             for tt in range(TOKEN_TILES):
                 nc.vector.tensor_scalar(
-                    out=z[:, tt, g, :, :].rearrange("p u (q r) -> p u q r", r=16),
-                    in0=x_mid[:, tt, cols].rearrange("p (q u r) -> p u q r", u=2, r=16),
+                    out=z[:, tt, g, :, :].rearrange("p u (q r) -> p u q r", r=run),
+                    in0=x_mid[:, tt, cols].rearrange("p (q u r) -> p u q r", u=2, r=run),
                     scalar1=mean_var[:, tt, 0:1],
                     scalar2=rstd[:, tt : tt + 1],
                     op0=ALU.subtract,
                     op1=ALU.mult,
                 )
-        order_block(last_out + 3)
+        transpose_block(LAST_OUT + 3)
 
         h_planes = const.tile([P, PASSES, PACK, TOKENS], BF16)
         for g in range(PASSES):
+            order = 0 if g < FC1_AS_IT_LIES else 1
             for u in range(2):
                 bank = bank_pool.tile([P, 2, 2, P], F32)
                 for e in range(2):
@@ -258,25 +264,33 @@ def tile_minitransformerlayer_pb_kernel(tc, h_attn, x, w_out, w_fc1, g2, b2, out
                         out=h_planes[:, g, 2 * u + e, :],
                         in_=bank[:, e, :, :].rearrange("p t j -> p (t j)"),
                         func=ACT.Identity,
-                        bias=bias[:, u, g, e : e + 1],
-                        scale=gain[:, u, g, e : e + 1],
+                        bias=gain_bias[:, order, u, PASSES + g, e : e + 1],
+                        scale=gain_bias[:, order, u, g, e : e + 1],
                     )
-        transpose_block(last_out + 3)
+
+        def interleave(g):
+            grouped = grouped_pool.tile([P, GROUP, PACK], BF16, align_bytes=64)
+            nc.vector.tensor_copy(out=grouped[:, :TOKENS, :], in_=h_planes[:, g, :, :].rearrange("p t n -> p n t"))
+            return grouped
+
+        quantise_group(GROUPS_OUT, range(0, 2))
         h_grouped = []
         for g in range(PASSES):
-            quantise_block(last_out + 2, [g])
-            grouped = grouped_pool.tile([P, BLOCK, PACK], BF16, align_bytes=64)
-            nc.vector.tensor_copy(out=grouped[:], in_=h_planes[:, g, :, :].rearrange("p t n -> p n t"))
-            h_grouped.append(grouped)
-            if g > 0:
-                quantise(h_grouped[g - 1], h_codes[:, g - 1, :], h_scales[:, g - 1, :])
-        order_block(last_out + 4)
-        quantise(h_grouped[PASSES - 1], h_codes[:, PASSES - 1, :], h_scales[:, PASSES - 1, :])
+            h_grouped.append(interleave(g))
+            if g < 2:
+                quantise_group(GROUPS_OUT, range(2 + g, 3 + g))
+            if g < PASSES - 1:
+                quantise(h_grouped[g][:, :TOKENS, :], h_codes[:, g, :], h_scales[:, g, :])
+        quantise(h_grouped[PASSES - 1][:, :TOKENS, :], h_codes[:, PASSES - 1, :], h_scales[:, PASSES - 1, :])
 
-        for b in range(last_out + 3, LAST_BLOCK + 1):
+        for i in range(GROUPS_OUT + 1, GROUPS):
+            b = 2 * i + 1
+            if i > GROUPS_OUT + 1:
+                transpose_block(b)
+                quantise_group(i - 1)
+            transpose_block(b + 1, vector_passes=(1,))
+            mlp(i - 1)
             order_block(b + 2)
-            transpose_block(b + 1, (1,) if b % 4 == 1 else ())
-            quantise_block(b)
-            mlp((b - 3) // 2, (b - 3) % 2)
-        for tt in range(TOKEN_TILES):
-            mlp(GROUPS - 1, tt)
+            order_block(b + 3)
+        quantise_group(GROUPS - 1)
+        mlp(GROUPS - 1)

@@ -26,9 +26,28 @@ GROUPS = GROUPS_OUT + D_FF // GROUP
 LAST_OUT = 2 * GROUPS_OUT
 LAST_BLOCK = 2 * GROUPS
 EPS = 1e-5
+COPY_RUN = 1
+COPY_FROM = 12
+Q_ACT = (2, 3, 0, 1)
+G_ORDER = (0, 1)
+LN12 = "S"
+LN13 = "V"
+LN14 = ""
+LNQ = 2
+X1, X2 = 4, 6
+OUT_ODD = "V"
+OUT_EVEN = "V"
+LN11 = "S"
+LN10 = "V"
+ACT_V1 = (1, 3)
+ACT_V0 = ()
+HEAD_PIECES = 2
+BY_PASS = (4,)
+Z_SCALAR = False
+LAST_V = (1,)
 
 RAW_BUFS = 8
-OUT_AS_IT_LIES = 4
+OUT_AS_IT_LIES = 3
 FC1_AS_IT_LIES = 1
 
 FLOPS = 2 * TOKENS * K * (D_MODEL + D_FF)
@@ -72,17 +91,22 @@ def tile_minitransformerlayer_pb_kernel(tc, h_attn, x, w_out, w_fc1, g2, b2, out
         def load_block(b):
             if b <= LAST_BLOCK:
                 raw = raw_pool.tile([P, 2, K], BF16)
-                nc.sync.dma_start(out=raw[:], in_=blocks[b].rearrange("(p c) k -> p c k", c=2))
+                rows = blocks[b].rearrange("(p c) k -> p c k", c=2)
+                pieces = HEAD_PIECES if b == 0 else 1
+                for n in range(pieces):
+                    ks = slice(n * K // pieces, (n + 1) * K // pieces)
+                    nc.sync.dma_start(out=raw[:, :, ks], in_=rows[:, :, ks])
                 raws[b] = raw
 
         x_sb = const.tile([P, TOKEN_TILES, D_MODEL], BF16)
         for b in range(RAW_BUFS):
             load_block(b)
-            if b >= 3 and b - 3 < GROUPS_OUT:
-                cols = slice((b - 3) * GROUP, (b - 2) * GROUP)
+            if b == 1:
+                nc.sync.dma_start(out=gain_rows[0:4, :], in_=g2.rearrange("(r c) -> r c", c=PACK * P))
+                nc.sync.dma_start(out=gain_rows[4:8, :], in_=b2.rearrange("(r c) -> r c", c=PACK * P))
+            if b in (X1, X2):
+                cols = slice((b > X1) * 2 * GROUP, (b > X1) * 2 * GROUP + 2 * GROUP)
                 nc.sync.dma_start(out=x_sb[:, :, cols], in_=x_rows[:, cols].rearrange("(t p) d -> p t d", p=P))
-        nc.sync.dma_start(out=gain_rows[0:4, :], in_=g2.rearrange("(r c) -> r c", c=PACK * P))
-        nc.sync.dma_start(out=gain_rows[4:8, :], in_=b2.rearrange("(r c) -> r c", c=PACK * P))
 
         sources = {}
 
@@ -110,6 +134,8 @@ def tile_minitransformerlayer_pb_kernel(tc, h_attn, x, w_out, w_fc1, g2, b2, out
             if b > LAST_BLOCK:
                 return
             i, half = divmod(b - 1, 2)
+            ready = []
+            run = COPY_RUN if b > COPY_FROM else 1
             for g in passes:
                 bank = bank_pool.tile([P, 2, 2, P], F32)
                 for c in range(2):
@@ -125,7 +151,11 @@ def tile_minitransformerlayer_pb_kernel(tc, h_attn, x, w_out, w_fc1, g2, b2, out
                 if g in vector_passes:
                     nc.vector.tensor_copy(out=to_words, in_=from_bank)
                 else:
-                    nc.scalar.copy(out=to_words, in_=from_bank)
+                    ready.append((to_words, from_bank))
+                if g % run == run - 1:
+                    for to_words, from_bank in reversed(ready):
+                        nc.scalar.copy(out=to_words, in_=from_bank)
+                    ready = []
             if PASSES - 1 in passes:
                 load_block(b + RAW_BUFS)
 
@@ -142,6 +172,16 @@ def tile_minitransformerlayer_pb_kernel(tc, h_attn, x, w_out, w_fc1, g2, b2, out
             codes, scales = weights[i]
             for g in passes:
                 quantise(grouped_tiles[i, g][:], codes[:, g, :], scales[:, g, :])
+
+        def quantise_half(i, half):
+            if i not in weights:
+                weight_codes = weight_pool.tile([P, PASSES, GROUP], U32, align_bytes=64)
+                weight_scales = weight_pool.tile([P, PASSES, GROUP], U8, align_bytes=64)
+                weights[i] = (weight_codes, weight_scales)
+            codes, scales = weights[i]
+            cols = slice(half * BLOCK, (half + 1) * BLOCK)
+            for g in range(PASSES):
+                quantise(grouped_tiles[i, g][:, cols, :], codes[:, g, cols], scales[:, g, cols])
 
         attn_codes = const.tile([P, PASSES, TOKENS], U32, align_bytes=64)
         attn_scales = const.tile([P, PASSES, TOKENS], U8, align_bytes=64)
@@ -177,10 +217,17 @@ def tile_minitransformerlayer_pb_kernel(tc, h_attn, x, w_out, w_fc1, g2, b2, out
 
         def mlp(i):
             cols = slice((i - GROUPS_OUT) * GROUP, (i - GROUPS_OUT + 1) * GROUP)
+            accs = []
             for tt in range(TOKEN_TILES):
                 acc = acc_pool.tile([P, GROUP], F32)
-                for g in range(PASSES):
-                    mx_pass(acc, (h_codes, h_scales), i, tt, g)
+                accs.append(acc)
+            order = [(tt, g) for tt in range(TOKEN_TILES) for g in range(PASSES)]
+            if i in BY_PASS:
+                order = [(tt, g) for g in range(PASSES) for tt in range(TOKEN_TILES)]
+            for tt, g in order:
+                mx_pass(accs[tt], (h_codes, h_scales), i, tt, g)
+            for tt in G_ORDER if i < GROUPS - 1 else (0, 1):
+                acc = accs[tt]
                 result = result_pool.tile([P, GROUP], F32)
                 nc.scalar.activation(out=result[:], in_=acc[:], func=ACT.Gelu)
                 nc.sync.dma_start(out=act_rows[tt * P : (tt + 1) * P, cols], in_=result[:])
@@ -193,14 +240,14 @@ def tile_minitransformerlayer_pb_kernel(tc, h_attn, x, w_out, w_fc1, g2, b2, out
         for i in range(GROUPS_OUT + 1):
             b = 2 * i + 1
             transpose_block(b)
-            order_block(b + 1)
+            order_block(b + 1, OUT_EVEN if i < GROUPS_OUT else LN10)
             if i > 0:
                 quantise_group(i - 1)
             if i > 1:
                 for tt in range(TOKEN_TILES):
                     measure(i - 2, tt)
             transpose_block(b + 1)
-            order_block(b + 2, "S")
+            order_block(b + 2, OUT_ODD if i < GROUPS_OUT - 1 else "V" if i < GROUPS_OUT else LN11)
             if i > 0:
                 for tt in range(TOKEN_TILES):
                     project(i - 1, tt)
@@ -234,7 +281,9 @@ def tile_minitransformerlayer_pb_kernel(tc, h_attn, x, w_out, w_fc1, g2, b2, out
         nc.vector.tensor_scalar_add(out=var_eps[:], in0=mean_var[:, :, 1], scalar1=EPS)
         rstd = const.tile([P, TOKEN_TILES], F32)
         nc.gpsimd.tensor_tensor(out=rstd[:], in0=var_eps[:], in1=minus_half[:], op=ALU.pow)
-        order_block(LAST_OUT + 4)
+        quantise_group(GROUPS_OUT, range(0, 1))
+        transpose_block(LAST_OUT + 3)
+        order_block(LAST_OUT + 4, LN12)
 
         z = const.tile([P, TOKEN_TILES, PASSES, 2, 2 * P], F32)
         for g in range(PASSES):
@@ -249,7 +298,6 @@ def tile_minitransformerlayer_pb_kernel(tc, h_attn, x, w_out, w_fc1, g2, b2, out
                     op0=ALU.subtract,
                     op1=ALU.mult,
                 )
-        transpose_block(LAST_OUT + 3)
 
         h_planes = const.tile([P, PASSES, PACK, TOKENS], BF16)
         for g in range(PASSES):
@@ -267,30 +315,37 @@ def tile_minitransformerlayer_pb_kernel(tc, h_attn, x, w_out, w_fc1, g2, b2, out
                         bias=gain_bias[:, order, u, PASSES + g, e : e + 1],
                         scale=gain_bias[:, order, u, g, e : e + 1],
                     )
+        transpose_block(LAST_OUT + 4)
+        order_block(LAST_OUT + 5, LN13)
+
+        h_grouped = const.tile([P, PASSES, TOKENS, PACK], BF16, align_bytes=64)
 
         def interleave(g):
-            grouped = grouped_pool.tile([P, GROUP, PACK], BF16, align_bytes=64)
-            nc.vector.tensor_copy(out=grouped[:, :TOKENS, :], in_=h_planes[:, g, :, :].rearrange("p t n -> p n t"))
-            return grouped
+            nc.vector.tensor_copy(out=h_grouped[:, g, :, :], in_=h_planes[:, g, :, :].rearrange("p t n -> p n t"))
 
-        quantise_group(GROUPS_OUT, range(0, 2))
-        h_grouped = []
+        quantise_group(GROUPS_OUT, range(1, LNQ))
         for g in range(PASSES):
-            h_grouped.append(interleave(g))
-            if g < 2:
-                quantise_group(GROUPS_OUT, range(2 + g, 3 + g))
+            interleave(g)
+            if g < PASSES - LNQ:
+                quantise_group(GROUPS_OUT, range(LNQ + g, LNQ + 1 + g))
             if g < PASSES - 1:
-                quantise(h_grouped[g][:, :TOKENS, :], h_codes[:, g, :], h_scales[:, g, :])
-        quantise(h_grouped[PASSES - 1][:, :TOKENS, :], h_codes[:, PASSES - 1, :], h_scales[:, PASSES - 1, :])
+                quantise(h_grouped[:, g, :, :], h_codes[:, g, :], h_scales[:, g, :])
+        if LN14 == "V":
+            order_block(LAST_OUT + 6)
+        quantise(h_grouped[:, PASSES - 1, :, :], h_codes[:, PASSES - 1, :], h_scales[:, PASSES - 1, :])
 
         for i in range(GROUPS_OUT + 1, GROUPS):
             b = 2 * i + 1
             if i > GROUPS_OUT + 1:
-                transpose_block(b)
-                quantise_group(i - 1)
-            transpose_block(b + 1, vector_passes=(1,))
+                transpose_block(b, vector_passes=ACT_V0)
+                quantise_group(i - 1, Q_ACT)
+            if i == GROUPS - 1:
+                quantise_half(i, 0)
+            if i > GROUPS_OUT + 1:
+                transpose_block(b + 1, vector_passes=ACT_V1 if i < GROUPS - 1 else LAST_V)
+                order_block(b + 2)
             mlp(i - 1)
-            order_block(b + 2)
-            order_block(b + 3)
-        quantise_group(GROUPS - 1)
+            if i > GROUPS_OUT + 1 or LN14 != "V":
+                order_block(b + 3)
+        quantise_half(GROUPS - 1, 1)
         mlp(GROUPS - 1)

@@ -26,7 +26,8 @@ GROUPS = GROUPS_OUT + D_FF // GROUP
 LAST_OUT = 2 * GROUPS_OUT
 LAST_BLOCK = 2 * GROUPS
 EPS = 1e-5
-COPY_RUN = 1
+BANKS = 6
+COPY_RUN = 2
 COPY_FROM = 12
 Q_ACT = (2, 3, 0, 1)
 G_ORDER = (0, 1)
@@ -39,7 +40,7 @@ OUT_ODD = "V"
 OUT_EVEN = "V"
 LN11 = "S"
 LN10 = "V"
-ACT_V1 = (1, 3)
+ACT_V1 = (1,)
 ACT_V0 = ()
 HEAD_PIECES = 2
 BY_PASS = (4,)
@@ -71,7 +72,7 @@ def tile_minitransformerlayer_pb_kernel(tc, h_attn, x, w_out, w_fc1, g2, b2, out
         grouped_pool = ctx.enter_context(tc.tile_pool(name="grouped", bufs=8))
         weight_pool = ctx.enter_context(tc.tile_pool(name="weights", bufs=4))
         result_pool = ctx.enter_context(tc.tile_pool(name="result", bufs=4))
-        bank_pool = ctx.enter_context(tc.psum_pool(name="banks", bufs=6))
+        bank_pool = ctx.enter_context(tc.psum_pool(name="banks", bufs=1))
         acc_pool = ctx.enter_context(tc.psum_pool(name="acc", bufs=2))
 
         zero = const.tile([P, 1], F32)
@@ -129,6 +130,13 @@ def tile_minitransformerlayer_pb_kernel(tc, h_attn, x, w_out, w_fc1, g2, b2, out
             sources[b].extend([ordered[:, :, :, g, :] for g in range(PASSES - first)])
 
         grouped_tiles = {}
+        free_banks = list(range(BANKS))
+
+        def new_bank(shape):
+            slot = free_banks[0]
+            free_banks.remove(slot)
+            bank = bank_pool.tile(shape, F32, name="bank" + str(slot))
+            return bank, slot
 
         def transpose_block(b, passes=range(PASSES), vector_passes=()):
             if b > LAST_BLOCK:
@@ -137,7 +145,7 @@ def tile_minitransformerlayer_pb_kernel(tc, h_attn, x, w_out, w_fc1, g2, b2, out
             ready = []
             run = COPY_RUN if b > COPY_FROM else 1
             for g in passes:
-                bank = bank_pool.tile([P, 2, 2, P], F32)
+                bank, slot = new_bank([P, 2, 2, P])
                 for c in range(2):
                     for u in range(2):
                         nc.tensor.transpose(bank[:, u, c, :], sources[b][g][:, u, c, :], ident[:])
@@ -150,11 +158,13 @@ def tile_minitransformerlayer_pb_kernel(tc, h_attn, x, w_out, w_fc1, g2, b2, out
                 from_bank = bank[:].rearrange("p u c j -> p j c u")
                 if g in vector_passes:
                     nc.vector.tensor_copy(out=to_words, in_=from_bank)
+                    free_banks.append(slot)
                 else:
-                    ready.append((to_words, from_bank))
+                    ready.append((to_words, from_bank, slot))
                 if g % run == run - 1:
-                    for to_words, from_bank in reversed(ready):
+                    for to_words, from_bank, slot in reversed(ready):
                         nc.scalar.copy(out=to_words, in_=from_bank)
+                        free_banks.append(slot)
                     ready = []
             if PASSES - 1 in passes:
                 load_block(b + RAW_BUFS)
@@ -258,12 +268,13 @@ def tile_minitransformerlayer_pb_kernel(tc, h_attn, x, w_out, w_fc1, g2, b2, out
                     in_=gain_rows[:].bitcast(F32).rearrange("p (q u i) -> p u q i", u=2, i=8),
                 )
             if i == 3:
-                bank = bank_pool.tile([P, 2, 2, P], F32)
+                bank, slot = new_bank([P, 2, 2, P])
                 for u in range(2):
                     nc.tensor.transpose(bank[:, 0, u, :], gain_rows[:].bitcast(F32)[:, u : 2 * P : 2], ident[:])
                     nc.tensor.transpose(bank[:, 1, u, :], gain_ordered[:, u, :], ident[:])
                 gain_words = const.tile([P, 2, 2, 8], F32)
                 nc.scalar.copy(out=gain_words[:], in_=bank[:, :, :, 0:8])
+                free_banks.append(slot)
                 gain_bias = const.tile([P, 2, 2, 8, 2], F32)
                 nc.vector.tensor_copy(
                     out=gain_bias[:].rearrange("p o u r e -> p (o u r e)"),
@@ -303,7 +314,7 @@ def tile_minitransformerlayer_pb_kernel(tc, h_attn, x, w_out, w_fc1, g2, b2, out
         for g in range(PASSES):
             order = 0 if g < FC1_AS_IT_LIES else 1
             for u in range(2):
-                bank = bank_pool.tile([P, 2, 2, P], F32)
+                bank, slot = new_bank([P, 2, 2, P])
                 for e in range(2):
                     for tt in range(TOKEN_TILES):
                         nc.tensor.transpose(bank[:, e, tt, :], z[:, tt, g, u, e : 2 * P : 2], ident[:])
@@ -315,6 +326,7 @@ def tile_minitransformerlayer_pb_kernel(tc, h_attn, x, w_out, w_fc1, g2, b2, out
                         bias=gain_bias[:, order, u, PASSES + g, e : e + 1],
                         scale=gain_bias[:, order, u, g, e : e + 1],
                     )
+                free_banks.append(slot)
         transpose_block(LAST_OUT + 4)
         order_block(LAST_OUT + 5, LN13)
 

@@ -26,6 +26,8 @@ GROUPS = GROUPS_OUT + D_FF // GROUP
 LAST_OUT = 2 * GROUPS_OUT
 LAST_BLOCK = 2 * GROUPS
 EPS = 1e-5
+LNF = 2
+HOP = range(15, 25, 2)
 BANKS = 6
 COPY_RUN = 2
 COPY_FROM = 12
@@ -69,6 +71,7 @@ def tile_minitransformerlayer_pb_kernel(tc, h_attn, x, w_out, w_fc1, g2, b2, out
         const = ctx.enter_context(tc.tile_pool(name="const", bufs=1))
         raw_pool = ctx.enter_context(tc.tile_pool(name="raw", bufs=RAW_BUFS))
         ordered_pool = ctx.enter_context(tc.tile_pool(name="ordered", bufs=3))
+        ordered_first_pool = ctx.enter_context(tc.tile_pool(name="ordered_first", bufs=1))
         grouped_pool = ctx.enter_context(tc.tile_pool(name="grouped", bufs=8))
         weight_pool = ctx.enter_context(tc.tile_pool(name="weights", bufs=4))
         result_pool = ctx.enter_context(tc.tile_pool(name="result", bufs=4))
@@ -128,6 +131,10 @@ def tile_minitransformerlayer_pb_kernel(tc, h_attn, x, w_out, w_fc1, g2, b2, out
             else:
                 nc.scalar.copy(out=to_runs, in_=from_runs)
             sources[b].extend([ordered[:, :, :, g, :] for g in range(PASSES - first)])
+            if b in HOP and first == 1:
+                ordered_first = ordered_first_pool.tile([P, 2, 2, P], F32)
+                nc.vector.tensor_copy(out=ordered_first[:], in_=as_it_lies[:, :, :, 0, :])
+                sources[b][0] = ordered_first[:]
 
         grouped_tiles = {}
         free_banks = list(range(BANKS))
@@ -281,18 +288,23 @@ def tile_minitransformerlayer_pb_kernel(tc, h_attn, x, w_out, w_fc1, g2, b2, out
                     in_=gain_words[:].rearrange("p o u r -> p (o u r)").bitcast(BF16),
                 )
         for tt in range(TOKEN_TILES):
-            measure(GROUPS_OUT - 1, tt)
-        for tt in range(TOKEN_TILES):
             nc.sync.dma_start(out=x_mid_rows[tt * P : (tt + 1) * P, :], in_=x_mid[:, tt, :])
 
         mean_var = const.tile([P, TOKEN_TILES, 2], F32)
+        var_eps = const.tile([P, TOKEN_TILES], F32)
+        rstd = const.tile([P, TOKEN_TILES], F32)
+        for tt in range(TOKEN_TILES):
+            measure(GROUPS_OUT - 1, tt)
         for tt in range(TOKEN_TILES):
             nc.vector.bn_aggr(out=mean_var[:, tt, :], in_=stats[:, tt, :, :].rearrange("p i s -> p (i s)"))
-        var_eps = const.tile([P, TOKEN_TILES], F32)
-        nc.vector.tensor_scalar_add(out=var_eps[:], in0=mean_var[:, :, 1], scalar1=EPS)
-        rstd = const.tile([P, TOKEN_TILES], F32)
-        nc.gpsimd.tensor_tensor(out=rstd[:], in0=var_eps[:], in1=minus_half[:], op=ALU.pow)
-        quantise_group(GROUPS_OUT, range(0, 1))
+        for tt in range(TOKEN_TILES):
+            nc.vector.tensor_scalar_add(
+                out=var_eps[:, tt : tt + 1], in0=mean_var[:, tt, 1:2], scalar1=EPS
+            )
+            nc.gpsimd.tensor_tensor(
+                out=rstd[:, tt : tt + 1], in0=var_eps[:, tt : tt + 1], in1=minus_half[:, tt : tt + 1], op=ALU.pow
+            )
+        quantise_group(GROUPS_OUT, range(0, LNF))
         transpose_block(LAST_OUT + 3)
         order_block(LAST_OUT + 4, LN12)
 
@@ -335,7 +347,7 @@ def tile_minitransformerlayer_pb_kernel(tc, h_attn, x, w_out, w_fc1, g2, b2, out
         def interleave(g):
             nc.vector.tensor_copy(out=h_grouped[:, g, :, :], in_=h_planes[:, g, :, :].rearrange("p t n -> p n t"))
 
-        quantise_group(GROUPS_OUT, range(1, LNQ))
+        quantise_group(GROUPS_OUT, range(LNF, LNQ))
         for g in range(PASSES):
             interleave(g)
             if g < PASSES - LNQ:

from contextlib import ExitStack

import concourse.mybir as mybir
from concourse.masks import make_identity

F32 = mybir.dt.float32
BF16 = mybir.dt.bfloat16
U32 = mybir.dt.uint32
U8 = mybir.dt.uint8
FP8X4 = mybir.dt.float8_e4m3fn_x4
ACT = mybir.ActivationFunctionType
ALU = mybir.AluOpType

P = 128
PACK = 4
K = 2048
PASSES = K // (P * PACK)
TOKENS = 256
TOKEN_TILES = TOKENS // P
D_MODEL = 2048
D_FF = 4096
BLOCK = 256
GROUP = 512
GROUPS_OUT = D_MODEL // GROUP
GROUPS = GROUPS_OUT + D_FF // GROUP
LAST_OUT = 2 * GROUPS_OUT
LAST_BLOCK = 2 * GROUPS
EPS = 1e-5
LNF = 2
HOP = range(15, 25, 2)
BANKS = 6
COPY_RUN = 2
COPY_FROM = 12
Q_ACT = (2, 3, 0, 1)
G_ORDER = (0, 1)
LN12 = "S"
LN13 = "V"
LN14 = ""
LNQ = 2
X1, X2 = 4, 6
OUT_ODD = "V"
OUT_EVEN = "V"
LN11 = "S"
LN10 = "V"
ACT_V1 = (1,)
ACT_V0 = ()
HEAD_PIECES = 2
BY_PASS = (4,)
Z_SCALAR = False
LAST_V = (1,)

RAW_BUFS = 8
OUT_AS_IT_LIES = 3
FC1_AS_IT_LIES = 1

FLOPS = 2 * TOKENS * K * (D_MODEL + D_FF)


def tile_minitransformerlayer_pb_kernel(tc, h_attn, x, w_out, w_fc1, g2, b2, out_0, out_1):
    nc = tc.nc
    x_rows = x.flatten_outer_dims()
    x_mid_rows = out_0.flatten_outer_dims()
    act_rows = out_1.flatten_outer_dims()

    blocks = [h_attn.flatten_outer_dims()]
    blocks.extend([w_out[r : r + BLOCK, :] for r in range(0, D_MODEL, BLOCK)])
    blocks.extend([w_fc1[r : r + BLOCK, :] for r in range(0, D_FF, BLOCK)])

    with ExitStack() as ctx:
        ctx.enter_context(tc.manual_schedule())
        const = ctx.enter_context(tc.tile_pool(name="const", bufs=1))
        raw_pool = ctx.enter_context(tc.tile_pool(name="raw", bufs=RAW_BUFS))
        ordered_pool = ctx.enter_context(tc.tile_pool(name="ordered", bufs=3))
        ordered_first_pool = ctx.enter_context(tc.tile_pool(name="ordered_first", bufs=1))
        grouped_pool = ctx.enter_context(tc.tile_pool(name="grouped", bufs=8))
        weight_pool = ctx.enter_context(tc.tile_pool(name="weights", bufs=4))
        result_pool = ctx.enter_context(tc.tile_pool(name="result", bufs=4))
        bank_pool = ctx.enter_context(tc.psum_pool(name="banks", bufs=1))
        acc_pool = ctx.enter_context(tc.psum_pool(name="acc", bufs=2))

        zero = const.tile([P, 1], F32)
        nc.vector.memset(zero[:], 0.0)
        table_warmer = const.tile([P, 1], F32)
        nc.scalar.activation(out=table_warmer[:], in_=zero[:], func=ACT.Gelu)

        ident = const.tile([P, P], F32)
        make_identity(nc, ident[:])
        minus_half = const.tile([P, TOKEN_TILES], F32)
        nc.gpsimd.memset(minus_half[:], -0.5)
        gain_rows = const.tile([P, PACK * P], BF16)
        nc.vector.memset(gain_rows[:], 0.0)

        raws = {}

        def load_block(b):
            if b <= LAST_BLOCK:
                raw = raw_pool.tile([P, 2, K], BF16)
                rows = blocks[b].rearrange("(p c) k -> p c k", c=2)
                pieces = HEAD_PIECES if b == 0 else 1
                for n in range(pieces):
                    ks = slice(n * K // pieces, (n + 1) * K // pieces)
                    nc.sync.dma_start(out=raw[:, :, ks], in_=rows[:, :, ks])
                raws[b] = raw

        x_sb = const.tile([P, TOKEN_TILES, D_MODEL], BF16)
        for b in range(RAW_BUFS):
            load_block(b)
            if b == 1:
                nc.sync.dma_start(out=gain_rows[0:4, :], in_=g2.rearrange("(r c) -> r c", c=PACK * P))
                nc.sync.dma_start(out=gain_rows[4:8, :], in_=b2.rearrange("(r c) -> r c", c=PACK * P))
            if b in (X1, X2):
                cols = slice((b > X1) * 2 * GROUP, (b > X1) * 2 * GROUP + 2 * GROUP)
                nc.sync.dma_start(out=x_sb[:, :, cols], in_=x_rows[:, cols].rearrange("(t p) d -> p t d", p=P))

        sources = {}

        def order_block(b, engine="V"):
            if b > LAST_BLOCK:
                return
            words = raws[b][:].bitcast(F32)
            first = OUT_AS_IT_LIES if b <= LAST_OUT else FC1_AS_IT_LIES
            as_it_lies = words.rearrange("p c (g w u) -> p u c g w", g=PASSES, u=2)
            sources[b] = [as_it_lies[:, :, :, g, :] for g in range(first)]
            if first == PASSES:
                return
            ordered = ordered_pool.tile([P, 2, 2, PASSES - first, P], F32)
            to_runs = ordered[:].rearrange("p u c g (q i) -> p u c (g q) i", i=8)
            from_runs = words[:, :, first * 2 * P :].rearrange("p c (a u i) -> p u c a i", u=2, i=8)
            if engine == "V":
                nc.vector.tensor_copy(out=to_runs, in_=from_runs)
            else:
                nc.scalar.copy(out=to_runs, in_=from_runs)
            sources[b].extend([ordered[:, :, :, g, :] for g in range(PASSES - first)])
            if b in HOP and first == 1:
                ordered_first = ordered_first_pool.tile([P, 2, 2, P], F32)
                nc.vector.tensor_copy(out=ordered_first[:], in_=as_it_lies[:, :, :, 0, :])
                sources[b][0] = ordered_first[:]

        grouped_tiles = {}
        free_banks = list(range(BANKS))

        def new_bank(shape):
            slot = free_banks[0]
            free_banks.remove(slot)
            bank = bank_pool.tile(shape, F32, name="bank" + str(slot))
            return bank, slot

        def transpose_block(b, passes=range(PASSES), vector_passes=()):
            if b > LAST_BLOCK:
                return
            i, half = divmod(b - 1, 2)
            ready = []
            run = COPY_RUN if b > COPY_FROM else 1
            for g in passes:
                bank, slot = new_bank([P, 2, 2, P])
                for c in range(2):
                    for u in range(2):
                        nc.tensor.transpose(bank[:, u, c, :], sources[b][g][:, u, c, :], ident[:])
                if (i, g) not in grouped_tiles:
                    grouped = grouped_pool.tile([P, GROUP, PACK], BF16, align_bytes=64)
                    grouped_tiles[i, g] = grouped
                start = half * BLOCK if b > 0 else 0
                columns = grouped_tiles[i, g][:, start : start + BLOCK, :]
                to_words = columns.bitcast(F32).rearrange("p (j c) u -> p j c u", c=2)
                from_bank = bank[:].rearrange("p u c j -> p j c u")
                if g in vector_passes:
                    nc.vector.tensor_copy(out=to_words, in_=from_bank)
                    free_banks.append(slot)
                else:
                    ready.append((to_words, from_bank, slot))
                if g % run == run - 1:
                    for to_words, from_bank, slot in reversed(ready):
                        nc.scalar.copy(out=to_words, in_=from_bank)
                        free_banks.append(slot)
                    ready = []
            if PASSES - 1 in passes:
                load_block(b + RAW_BUFS)

        def quantise(grouped, codes, scales):
            nc.vector.quantize_mx(out=codes.bitcast(FP8X4), scales=scales, in_=grouped.rearrange("p n t -> p (n t)"))

        weights = {}

        def quantise_group(i, passes=range(PASSES)):
            if i not in weights:
                weight_codes = weight_pool.tile([P, PASSES, GROUP], U32, align_bytes=64)
                weight_scales = weight_pool.tile([P, PASSES, GROUP], U8, align_bytes=64)
                weights[i] = (weight_codes, weight_scales)
            codes, scales = weights[i]
            for g in passes:
                quantise(grouped_tiles[i, g][:], codes[:, g, :], scales[:, g, :])

        def quantise_half(i, half):
            if i not in weights:
                weight_codes = weight_pool.tile([P, PASSES, GROUP], U32, align_bytes=64)
                weight_scales = weight_pool.tile([P, PASSES, GROUP], U8, align_bytes=64)
                weights[i] = (weight_codes, weight_scales)
            codes, scales = weights[i]
            cols = slice(half * BLOCK, (half + 1) * BLOCK)
            for g in range(PASSES):
                quantise(grouped_tiles[i, g][:, cols, :], codes[:, g, cols], scales[:, g, cols])

        attn_codes = const.tile([P, PASSES, TOKENS], U32, align_bytes=64)
        attn_scales = const.tile([P, PASSES, TOKENS], U8, align_bytes=64)
        h_codes = const.tile([P, PASSES, TOKENS], U32, align_bytes=64)
        h_scales = const.tile([P, PASSES, TOKENS], U8, align_bytes=64)

        def mx_pass(acc, tokens, i, tt, g):
            token_codes, token_scales = tokens
            weight_codes, weight_scales = weights[i]
            rows = slice(tt * P, (tt + 1) * P)
            nc.tensor.matmul_mx(
                out=acc[:],
                lhsT=token_codes[:, g, rows].bitcast(FP8X4),
                lhsT_scale=token_scales[:, g, rows],
                rhs=weight_codes[:, g, :].bitcast(FP8X4),
                rhs_scale=weight_scales[:, g, :],
                start=(g == 0),
                stop=(g == PASSES - 1),
            )

        x_mid = const.tile([P, TOKEN_TILES, D_MODEL], F32)
        stats = const.tile([P, TOKEN_TILES, GROUPS_OUT, 6], F32)

        def project(i, tt):
            cols = slice(i * GROUP, (i + 1) * GROUP)
            acc = acc_pool.tile([P, GROUP], F32)
            for g in range(PASSES):
                mx_pass(acc, (attn_codes, attn_scales), i, tt, g)
            nc.vector.tensor_tensor(out=x_mid[:, tt, cols], in0=acc[:], in1=x_sb[:, tt, cols], op=ALU.add)

        def measure(i, tt):
            nc.vector.bn_stats(out=stats[:, tt, i, :], in_=x_mid[:, tt, i * GROUP : (i + 1) * GROUP])

        def mlp(i):
            cols = slice((i - GROUPS_OUT) * GROUP, (i - GROUPS_OUT + 1) * GROUP)
            accs = []
            for tt in range(TOKEN_TILES):
                acc = acc_pool.tile([P, GROUP], F32)
                accs.append(acc)
            order = [(tt, g) for tt in range(TOKEN_TILES) for g in range(PASSES)]
            if i in BY_PASS:
                order = [(tt, g) for g in range(PASSES) for tt in range(TOKEN_TILES)]
            for tt, g in order:
                mx_pass(accs[tt], (h_codes, h_scales), i, tt, g)
            for tt in G_ORDER if i < GROUPS - 1 else (0, 1):
                acc = accs[tt]
                result = result_pool.tile([P, GROUP], F32)
                nc.scalar.activation(out=result[:], in_=acc[:], func=ACT.Gelu)
                nc.sync.dma_start(out=act_rows[tt * P : (tt + 1) * P, cols], in_=result[:])

        order_block(0)
        transpose_block(0)
        order_block(1)
        for g in range(PASSES):
            quantise(grouped_tiles[-1, g][:, :BLOCK, :], attn_codes[:, g, :], attn_scales[:, g, :])
        for i in range(GROUPS_OUT + 1):
            b = 2 * i + 1
            transpose_block(b)
            order_block(b + 1, OUT_EVEN if i < GROUPS_OUT else LN10)
            if i > 0:
                quantise_group(i - 1)
            if i > 1:
                for tt in range(TOKEN_TILES):
                    measure(i - 2, tt)
            transpose_block(b + 1)
            order_block(b + 2, OUT_ODD if i < GROUPS_OUT - 1 else "V" if i < GROUPS_OUT else LN11)
            if i > 0:
                for tt in range(TOKEN_TILES):
                    project(i - 1, tt)
            if i == 2:
                gain_ordered = const.tile([P, 2, P], F32)
                nc.vector.tensor_copy(
                    out=gain_ordered[:].rearrange("p u (q i) -> p u q i", i=8),
                    in_=gain_rows[:].bitcast(F32).rearrange("p (q u i) -> p u q i", u=2, i=8),
                )
            if i == 3:
                bank, slot = new_bank([P, 2, 2, P])
                for u in range(2):
                    nc.tensor.transpose(bank[:, 0, u, :], gain_rows[:].bitcast(F32)[:, u : 2 * P : 2], ident[:])
                    nc.tensor.transpose(bank[:, 1, u, :], gain_ordered[:, u, :], ident[:])
                gain_words = const.tile([P, 2, 2, 8], F32)
                nc.scalar.copy(out=gain_words[:], in_=bank[:, :, :, 0:8])
                free_banks.append(slot)
                gain_bias = const.tile([P, 2, 2, 8, 2], F32)
                nc.vector.tensor_copy(
                    out=gain_bias[:].rearrange("p o u r e -> p (o u r e)"),
                    in_=gain_words[:].rearrange("p o u r -> p (o u r)").bitcast(BF16),
                )
        for tt in range(TOKEN_TILES):
            nc.sync.dma_start(out=x_mid_rows[tt * P : (tt + 1) * P, :], in_=x_mid[:, tt, :])

        mean_var = const.tile([P, TOKEN_TILES, 2], F32)
        var_eps = const.tile([P, TOKEN_TILES], F32)
        rstd = const.tile([P, TOKEN_TILES], F32)
        for tt in range(TOKEN_TILES):
            measure(GROUPS_OUT - 1, tt)
        for tt in range(TOKEN_TILES):
            nc.vector.bn_aggr(out=mean_var[:, tt, :], in_=stats[:, tt, :, :].rearrange("p i s -> p (i s)"))
        for tt in range(TOKEN_TILES):
            nc.vector.tensor_scalar_add(
                out=var_eps[:, tt : tt + 1], in0=mean_var[:, tt, 1:2], scalar1=EPS
            )
            nc.gpsimd.tensor_tensor(
                out=rstd[:, tt : tt + 1], in0=var_eps[:, tt : tt + 1], in1=minus_half[:, tt : tt + 1], op=ALU.pow
            )
        quantise_group(GROUPS_OUT, range(0, LNF))
        transpose_block(LAST_OUT + 3)
        order_block(LAST_OUT + 4, LN12)

        z = const.tile([P, TOKEN_TILES, PASSES, 2, 2 * P], F32)
        for g in range(PASSES):
            run = 2 if g < FC1_AS_IT_LIES else 16
            cols = slice(g * P * PACK, (g + 1) * P * PACK)
            for tt in range(TOKEN_TILES):
                nc.vector.tensor_scalar(
                    out=z[:, tt, g, :, :].rearrange("p u (q r) -> p u q r", r=run),
                    in0=x_mid[:, tt, cols].rearrange("p (q u r) -> p u q r", u=2, r=run),
                    scalar1=mean_var[:, tt, 0:1],
                    scalar2=rstd[:, tt : tt + 1],
                    op0=ALU.subtract,
                    op1=ALU.mult,
                )

        h_planes = const.tile([P, PASSES, PACK, TOKENS], BF16)
        for g in range(PASSES):
            order = 0 if g < FC1_AS_IT_LIES else 1
            for u in range(2):
                bank, slot = new_bank([P, 2, 2, P])
                for e in range(2):
                    for tt in range(TOKEN_TILES):
                        nc.tensor.transpose(bank[:, e, tt, :], z[:, tt, g, u, e : 2 * P : 2], ident[:])
                for e in range(2):
                    nc.scalar.activation(
                        out=h_planes[:, g, 2 * u + e, :],
                        in_=bank[:, e, :, :].rearrange("p t j -> p (t j)"),
                        func=ACT.Identity,
                        bias=gain_bias[:, order, u, PASSES + g, e : e + 1],
                        scale=gain_bias[:, order, u, g, e : e + 1],
                    )
                free_banks.append(slot)
        transpose_block(LAST_OUT + 4)
        order_block(LAST_OUT + 5, LN13)

        h_grouped = const.tile([P, PASSES, TOKENS, PACK], BF16, align_bytes=64)

        def interleave(g):
            nc.vector.tensor_copy(out=h_grouped[:, g, :, :], in_=h_planes[:, g, :, :].rearrange("p t n -> p n t"))

        quantise_group(GROUPS_OUT, range(LNF, LNQ))
        for g in range(PASSES):
            interleave(g)
            if g < PASSES - LNQ:
                quantise_group(GROUPS_OUT, range(LNQ + g, LNQ + 1 + g))
            if g < PASSES - 1:
                quantise(h_grouped[:, g, :, :], h_codes[:, g, :], h_scales[:, g, :])
        if LN14 == "V":
            order_block(LAST_OUT + 6)
        quantise(h_grouped[:, PASSES - 1, :, :], h_codes[:, PASSES - 1, :], h_scales[:, PASSES - 1, :])

        for i in range(GROUPS_OUT + 1, GROUPS):
            b = 2 * i + 1
            if i > GROUPS_OUT + 1:
                transpose_block(b, vector_passes=ACT_V0)
                quantise_group(i - 1, Q_ACT)
            if i == GROUPS - 1:
                quantise_half(i, 0)
            if i > GROUPS_OUT + 1:
                transpose_block(b + 1, vector_passes=ACT_V1 if i < GROUPS - 1 else LAST_V)
                order_block(b + 2)
            mlp(i - 1)
            if i > GROUPS_OUT + 1 or LN14 != "V":
                order_block(b + 3)
        quantise_half(GROUPS - 1, 1)
        mlp(GROUPS - 1)
